import numpy as np
import ml_dtypes


def mxq(x, axis, fmt="e4m3"):
    dtype, down = {"e4m3": (ml_dtypes.float8_e4m3fn, 7), "e5m2": (ml_dtypes.float8_e5m2, 14)}[fmt]
    v = np.moveaxis(np.asarray(x, np.float32).astype(ml_dtypes.bfloat16).astype(np.float64), axis, -1)
    blocks = v.reshape(v.shape[:-1] + (-1, 32))
    amax = np.abs(blocks).max(-1, keepdims=True)
    byte = np.maximum(np.where(amax > 0, np.frexp(amax)[1] - 1 + 127, 0) - down, 1)
    scale = np.exp2(byte - 127.0)
    codes = (blocks / scale).astype(np.float32).astype(dtype).astype(np.float64)
    return np.moveaxis((codes * scale).reshape(v.shape), -1, axis)


WIDE = False


def mx_kscale(k):
    if not WIDE:
        return np.ones(k)
    levels = np.array([10, -10, 5, -5, 0])
    if k % 512:
        return np.exp2(np.random.permutation(np.resize(levels, k // 32))).repeat(32)
    a = np.empty((k // 512, 16))
    for p in range(k // 512):
        a[p, :8] = np.random.permutation(np.resize(levels, 8))
        for g in range(8):
            far = levels[np.abs(levels - a[p, g]) >= 10]
            a[p, g + 8] = far[np.random.randint(len(far))]
    return np.exp2(a.ravel()).repeat(32)


BF16 = ml_dtypes.bfloat16


def bf(x):
    return np.asarray(x, np.float32).astype(BF16)


def f64(x):
    return np.asarray(x).astype(np.float64)


B, J, C, K, H = 8, 128, 512, 4, 256
KJ = K * J
EPS = 1e-5


def layernorm(v, g, b):
    m = v.mean(-1, keepdims=True)
    var = v.var(-1, keepdims=True)
    return (v - m) / np.sqrt(var + EPS) * g + b


def gcn(xin, adj, spatial_adj, conv_w, conv_b, s_ctx):
    h = f64(bf(mxq(xin, 2, "e4m3") @ mxq(conv_w, 1, "e4m3").T)) + conv_b
    h = h.reshape(B, J, K, C).transpose(0, 2, 1, 3).reshape(B, KJ, C)
    sadj = np.broadcast_to(spatial_adj[None], (B, K - 1, J, J))
    adj4 = np.concatenate([adj * s_ctx, sadj], axis=1).reshape(B, KJ, J)
    return mxq(adj4, 1, "e4m3").transpose(0, 2, 1) @ mxq(h, 1, "e4m3")


def setup_inputs():
    s = mx_kscale(C)
    t = np.sort(mx_kscale(KJ))[np.arange(K) * (KJ - 1) // (K - 1)]
    tw = np.repeat(t, C)
    a = 2.0 / np.sqrt(KJ)
    return {"g1": bf(np.random.standard_normal((B, J, C)) * 0.9 * s),
            "res1": bf(np.random.standard_normal((B, J, C))),
            "adj": bf(np.random.random((B, 1, J, J)) * a / t[0]),
            "spatial_adj": bf(np.random.random((K - 1, J, J)) * a / t[1:, None, None]),
            "conv2_w": bf(np.random.standard_normal((K * C, C)) / np.sqrt(C) / s[None, :] * tw[:, None]),
            "conv2_b": bf(np.random.standard_normal(K * C) * 0.05 * tw),
            "s2": bf(1.5 + 0.1 * np.random.standard_normal(1)),
            "norm2_g": bf(1.0 + 0.1 * np.random.standard_normal(C)),
            "norm2_b": bf(0.1 * np.random.standard_normal(C))}


def reference(g1, res1, adj, spatial_adj, conv2_w, conv2_b, s2, norm2_g, norm2_b):
    g2 = gcn(f64(g1), f64(adj), f64(spatial_adj), f64(conv2_w), f64(conv2_b), f64(s2))
    x2 = f64(res1) + g2
    xn = layernorm(x2, f64(norm2_g), f64(norm2_b))
    return x2, xn

@@ -1,0 +1,328 @@
+from contextlib import ExitStack
+
+import concourse.masks as masks
+import concourse.mybir as mybir
+
+F32 = mybir.dt.float32
+BF16 = mybir.dt.bfloat16
+U32 = mybir.dt.uint32
+U8 = mybir.dt.uint8
+FP8X4 = mybir.dt.float8_e4m3fn_x4
+ALU = mybir.AluOpType
+ACT = mybir.ActivationFunctionType
+
+B, J, C, K = 8, 128, 512, 4
+EPS = 1e-5
+P = 128
+HALF = 4
+BANK_DT = BF16
+
+FLOPS = 2 * B * J * C * K * C + 2 * B * J * K * J * C
+
+ON_VECTOR = {(0, 0): (2, 3), (0, 1): (2, 3), (1, 0): (3,), (1, 1): (1, 2, 3)}
+WARM_UP = 6
+
+
+def tile_block_attention_guide_pb_kernel(tc, g1, res1, adj, spatial_adj, conv2_w, conv2_b, s2, norm2_g, norm2_b, out_0, out_1):
+    nc = tc.nc
+    with ExitStack() as ctx:
+        keep = ctx.enter_context(tc.tile_pool(name="keep", bufs=1))
+        work = ctx.enter_context(tc.tile_pool(name="work", bufs=3))
+        psum = ctx.enter_context(tc.psum_pool(name="psum", bufs=8))
+        ctx.enter_context(tc.manual_schedule())
+
+        g_sb = [keep.tile([P, HALF, C], BF16, name="g_sb%d" % h) for h in range(2)]
+        w_sb = [keep.tile([P, 4, C], BF16, name="w_sb%d" % q) for q in range(K)]
+        a_raw = keep.tile([P, B, 4, J], BF16, name="a_raw")
+        res_sb = keep.tile([P, B, C], BF16, name="res_sb")
+        b_rows = keep.tile([P, P], BF16, name="b_rows")
+        gb_rows = keep.tile([P, 2 * C], BF16, name="gb_rows")
+        gain = keep.tile([P, 1], BF16, name="gain")
+        ones = keep.tile([P, P], BF16, name="ones")
+        idle = keep.tile([P, C], BF16, name="idle")
+        warm = keep.tile([P, 1], F32, name="warm")
+        warm2 = keep.tile([P, 1], F32, name="warm2")
+        gam = keep.tile([P, C], BF16, name="gam")
+        bet = keep.tile([P, C], BF16, name="bet")
+        ident_f = keep.tile([P, P], F32, name="ident_f")
+        perm_f = keep.tile([P, P], F32, name="perm_f")
+        ident_b = keep.tile([P, P], BF16, name="ident_b")
+        bias_f = keep.tile([P, 16], F32, name="bias_f")
+        g_in = [keep.tile([P, 4 * C], BF16, name="g_in%d" % h, align_bytes=64) for h in range(2)]
+        g_q = [keep.tile([P, C], U32, name="g_q%d" % h, align_bytes=64) for h in range(2)]
+        g_s = [keep.tile([P, C], U8, name="g_s%d" % h, align_bytes=64) for h in range(2)]
+        w_in = [keep.tile([P, 4 * C], BF16, name="w_in%d" % q, align_bytes=64) for q in range(K)]
+        w_q = [keep.tile([P, C], U32, name="w_q%d" % q, align_bytes=64) for q in range(K)]
+        w_s = [keep.tile([P, C], U8, name="w_s%d" % q, align_bytes=64) for q in range(K)]
+        a_in = [keep.tile([P, HALF * J * 4], BF16, name="a_in%d" % h, align_bytes=64) for h in range(2)]
+        a_q = [keep.tile([P, HALF * J], U32, name="a_q%d" % h, align_bytes=64) for h in range(2)]
+        a_s = [keep.tile([P, HALF * J], U8, name="a_s%d" % h, align_bytes=64) for h in range(2)]
+        h_t = [[keep.tile([P, HALF * C], BF16, name="h_t%d_%d" % (h, j)) for j in range(4)] for h in range(2)]
+        live = {}
+
+        nc.vector.memset(ones[:], 1.0)
+        nc.vector.memset(idle[:], 0.0)
+        nc.vector.memset(gb_rows[:], 0.0)
+        nc.vector.memset(b_rows[:], 0.0)
+        nc.vector.memset(gain[:], 1.0)
+        nc.vector.memset(warm[:], 1.0)
+        nc.scalar.dma_start(out=gb_rows[0:1, 0:C], in_=norm2_g.rearrange("(o c) -> o c", o=1))
+        nc.scalar.dma_start(out=gb_rows[0:1, C : 2 * C], in_=norm2_b.rearrange("(o c) -> o c", o=1))
+        nc.scalar.dma_start(out=b_rows[0:16, :], in_=conv2_b.rearrange("(j p) -> j p", p=P))
+        nc.scalar.activation(out=warm2[:], in_=warm[:], func=ACT.Abs_reciprocal_sqrt)
+
+        def load_g(h, lo, hi):
+            nc.sync.dma_start(out=g_sb[h][:, lo:hi, :], in_=g1[HALF * h + lo : HALF * h + hi].rearrange("b v c -> v b c"))
+
+        def load_w(q, lo, hi):
+            nc.sync.dma_start(
+                out=w_sb[q][:, lo:hi, :],
+                in_=conv2_w[C * q + P * lo : C * q + P * hi, :].rearrange("(j p) c -> p j c", p=P),
+            )
+
+        load_g(0, 0, 2)
+        load_g(0, 2, 4)
+        load_w(0, 0, 2)
+        load_w(0, 2, 4)
+        load_w(1, 0, 4)
+        load_w(2, 0, 4)
+        load_w(3, 0, 4)
+        load_g(1, 0, 4)
+        nc.sync.dma_start(out=gain[0:32, :], in_=s2.partition_broadcast(32))
+        for h in range(2):
+            some = slice(HALF * h, HALF * (h + 1))
+            nc.sync.dma_start(
+                out=a_raw[32:128, some].rearrange("p b t w -> p b (t w)"),
+                in_=spatial_adj.rearrange("k (m t) w -> (k m) (t w)", t=4).unsqueeze(1).to_broadcast([96, HALF, 4 * J]),
+            )
+            nc.sync.dma_start(out=a_raw[0:32, some], in_=adj[some].rearrange("b o (m t) w -> m (b o) t w", t=4))
+        for h in range(2):
+            some = slice(HALF * h, HALF * (h + 1))
+            nc.sync.dma_start(out=res_sb[:, some, :], in_=res1[some].rearrange("b w c -> w b c"))
+
+        masks.make_identity(nc, ident_f[:])
+        nc.vector.tensor_copy(
+            out=perm_f[:].rearrange("p (u m e) -> p u m e", u=2, e=2),
+            in_=ident_f[:].rearrange("p (m u e) -> p u m e", u=2, e=2),
+        )
+        nc.vector.tensor_copy(out=ident_b[:], in_=ident_f[:])
+
+        def bank_tile(shape, dtype):
+            return psum.tile(shape, dtype, name="ps", tag="ps")
+
+        def spin():
+            nc.tensor.matmul(out=bank_tile([P, C], F32)[:], lhsT=ones[:], rhs=idle[:], start=True, stop=True)
+
+        def spread(i):
+            wide = bank_tile([P, C], F32)
+            nc.tensor.matmul(out=wide[:], lhsT=ones[:], rhs=gb_rows[:, C * i : C * (i + 1)], start=True, stop=True)
+            live[("wide", i)] = wide
+
+        def keep_spread(i, vec):
+            nc.scalar.copy(out=vec[:], in_=live[("wide", i)][:])
+
+        def copy_words(eng, dst, src):
+            if eng == "V":
+                nc.vector.tensor_copy(out=dst, in_=src)
+            else:
+                nc.scalar.copy(out=dst, in_=src)
+
+        def turn_rows(key, rows, ident, pair):
+            tr = bank_tile([P, 2, 2, P], F32)
+            for a in range(2):
+                words = rows[:, 2 * pair + a, :].bitcast(F32)
+                for u in range(2):
+                    nc.tensor.transpose(tr[:, a, u, :], words[:, u::2], ident[:])
+            live[key] = tr
+
+        def empty_rows(key, grouped, pair, eng):
+            dst = grouped[:].bitcast(F32).rearrange("p (a r u) -> p a r u", a=4, u=2)
+            copy_words(eng, dst[:, 2 * pair : 2 * pair + 2], live[key][:].rearrange("p a u r -> p a r u"))
+
+        def quantize(codes, scales, grouped):
+            nc.vector.quantize_mx(out=codes[:].bitcast(FP8X4), scales=scales[:], in_=grouped[:])
+
+        def turn_bias():
+            b_t = bank_tile([P, P], BF16)
+            nc.tensor.transpose(b_t[:], b_rows[:], ident_b[:])
+            nc.vector.tensor_copy(out=bias_f[:], in_=b_t[:, 0:16])
+
+        def stage1(q, j, h):
+            bank = bank_tile([P, HALF * J], BANK_DT)
+            cols = slice(P * j, P * (j + 1))
+            nc.tensor.matmul_mx(
+                out=bank[:],
+                lhsT=w_q[q][:, cols].bitcast(FP8X4),
+                lhsT_scale=w_s[q][:, cols],
+                rhs=g_q[h][:].bitcast(FP8X4),
+                rhs_scale=g_s[h][:],
+                start=True,
+                stop=True,
+            )
+            live[("bank", q, j, h)] = bank
+
+        def empty_bank(q, j, h):
+            bank = live[("bank", q, j, h)]
+            dst = h_t[h][j][:].rearrange("p (b u k x) -> p b u k x", b=HALF, u=2, k=K)[:, :, :, q, :]
+            src = bank[:].rearrange("p (b u x) -> p b u x", b=HALF, u=2)
+            col = bias_f[:, 4 * q + j : 4 * q + j + 1]
+            if j in ON_VECTOR[(h, q % 2)]:
+                nc.vector.tensor_scalar(out=dst, in0=src, scalar1=col, scalar2=None, op0=ALU.add)
+            else:
+                nc.scalar.activation(out=dst, in_=src, func=ACT.Identity, bias=col, scale=1.0)
+
+        def turn_h(b, pair):
+            h, bl = divmod(b, HALF)
+            tr = bank_tile([P, 2, 2, P], F32)
+            for a in range(2):
+                rows = h_t[h][2 * pair + a][:].rearrange("p (b u x) -> p b u x", b=HALF, u=2)
+                for u in range(2):
+                    nc.tensor.transpose(tr[:, a, u, :], rows[:, bl, u, :].bitcast(F32), ident_f[:])
+            live[("h", b, pair)] = tr
+
+        def empty_h(b, pair):
+            if pair == 0:
+                h_in = work.tile([P, 4 * C], BF16, name="h_in", tag="h_in", align_bytes=64)
+                live[("h_in", b)] = h_in
+            empty_rows(("h", b, pair), live[("h_in", b)], pair, "S")
+
+        def quantize_h(b):
+            h_q = work.tile([P, C], U32, name="h_q", tag="h_q", align_bytes=64)
+            h_s = work.tile([P, C], U8, name="h_s", tag="h_s", align_bytes=64)
+            quantize(h_q, h_s, live[("h_in", b)])
+            live[("h_q", b)] = (h_q, h_s)
+
+        def adjacency(h):
+            nc.vector.tensor_scalar(
+                out=a_in[h][:].rearrange("p (b w t) -> p b w t", b=HALF, t=4),
+                in0=a_raw[:, HALF * h : HALF * (h + 1)].rearrange("p b t w -> p b w t"),
+                scalar1=gain[:, 0:1],
+                scalar2=None,
+                op0=ALU.mult,
+            )
+            quantize(a_q[h], a_s[h], a_in[h])
+
+        def stage2(b):
+            h, bl = divmod(b, HALF)
+            h_q, h_s = live[("h_q", b)]
+            acc = bank_tile([P, C], F32)
+            cols = slice(J * bl, J * (bl + 1))
+            nc.tensor.matmul_mx(
+                out=acc[:],
+                lhsT=a_q[h][:, cols].bitcast(FP8X4),
+                lhsT_scale=a_s[h][:, cols],
+                rhs=h_q[:].bitcast(FP8X4),
+                rhs_scale=h_s[:],
+                start=True,
+                stop=True,
+            )
+            live[("acc", b)] = acc
+
+        def residual(b):
+            x2 = work.tile([P, C], F32, name="x2", tag="x2")
+            total = work.tile([P, 1], F32, name="total", tag="total")
+            nc.vector.scalar_tensor_tensor(
+                out=x2[:], in0=live[("acc", b)][:], scalar=1.0, in1=res_sb[:, b, :],
+                op0=ALU.mult, op1=ALU.add, accum_out=total[:],
+            )
+            nc.sync.dma_start(out=out_0[b], in_=x2[:])
+            negm = work.tile([P, 1], F32, name="negm", tag="negm")
+            nc.scalar.activation(out=negm[:], in_=total[:], func=ACT.Copy, scale=-1.0 / C)
+            live[("x2", b)] = (x2, total, negm)
+
+        def spread_of(b):
+            x2, total, negm = live[("x2", b)]
+            junk = work.tile([P, C], BF16, name="junk", tag="junk")
+            ssq = work.tile([P, 1], F32, name="ssq", tag="ssq")
+            nc.scalar.activation(
+                out=junk[:], in_=x2[:], func=ACT.Square, bias=total[:, 0:1], scale=-1.0 * C, accum_out=ssq[:]
+            )
+            rstd = work.tile([P, 1], F32, name="rstd", tag="rstd")
+            nc.scalar.activation(
+                out=rstd[:], in_=ssq[:], func=ACT.Abs_reciprocal_sqrt, bias=EPS, scale=1.0 / (C * C * C)
+            )
+            live[("rstd", b)] = rstd
+
+        def centre(b):
+            x2, total, negm = live[("x2", b)]
+            cen = work.tile([P, C], F32, name="cen", tag="cen")
+            nc.vector.scalar_tensor_tensor(
+                out=cen[:], in0=x2[:], scalar=negm[:, 0:1], in1=gam[:], op0=ALU.add, op1=ALU.mult
+            )
+            live[("cen", b)] = cen
+
+        def finish(b):
+            xn = work.tile([P, C], F32, name="xn", tag="xn")
+            nc.vector.scalar_tensor_tensor(
+                out=xn[:], in0=live[("cen", b)][:], scalar=live[("rstd", b)][:, 0:1], in1=bet[:],
+                op0=ALU.mult, op1=ALU.add,
+            )
+            nc.sync.dma_start(out=out_1[b], in_=xn[:])
+
+        for i in range(WARM_UP):
+            spin()
+
+        turn_rows(("g", 0, 0), g_sb[0], perm_f, 0)
+        turn_rows(("g", 0, 1), g_sb[0], perm_f, 1)
+        spread(0)
+        turn_bias()
+        empty_rows(("g", 0, 0), g_in[0], 0, "S")
+        empty_rows(("g", 0, 1), g_in[0], 1, "V")
+        keep_spread(0, gam)
+        quantize(g_q[0], g_s[0], g_in[0])
+        turn_rows(("w", 0, 0), w_sb[0], ident_f, 0)
+        spread(1)
+        turn_rows(("w", 0, 1), w_sb[0], ident_f, 1)
+        spin()
+        empty_rows(("w", 0, 0), w_in[0], 0, "S")
+        empty_rows(("w", 0, 1), w_in[0], 1, "V")
+        keep_spread(1, bet)
+        quantize(w_q[0], w_s[0], w_in[0])
+        for q in range(1, K + 1):
+            for pair in range(2):
+                if q < K:
+                    turn_rows(("w", q, pair), w_sb[q], ident_f, pair)
+                else:
+                    turn_rows(("g", 1, pair), g_sb[1], perm_f, pair)
+                if q == 1:
+                    spin()
+            for j in range(4):
+                stage1(q - 1, j, 0)
+            if q < K:
+                empty_rows(("w", q, 0), w_in[q], 0, "S")
+                empty_rows(("w", q, 1), w_in[q], 1, "V")
+                quantize(w_q[q], w_s[q], w_in[q])
+            else:
+                empty_rows(("g", 1, 0), g_in[1], 0, "S")
+                empty_rows(("g", 1, 1), g_in[1], 1, "V")
+                quantize(g_q[1], g_s[1], g_in[1])
+            for j in range(4):
+                empty_bank(q - 1, j, 0)
+
+        for i in range(B + 4):
+            late = (2 * i, 2 * i + 1) if i < 2 else ()
+            if i < B:
+                for pair in range(2):
+                    turn_h(i, pair)
+                for pair in range(2):
+                    empty_h(i, pair)
+            for q in late:
+                for j in range(4):
+                    stage1(q, j, 1)
+            if i == 0:
+                adjacency(0)
+                adjacency(1)
+            if 0 <= i - 1 < B:
+                quantize_h(i - 1)
+                stage2(i - 1)
+            if 0 <= i - 3 < B:
+                spread_of(i - 3)
+            for q in late:
+                for j in range(4):
+                    empty_bank(q, j, 1)
+            if 0 <= i - 2 < B:
+                residual(i - 2)
+            if 0 <= i - 3 < B:
+                centre(i - 3)
+            if 0 <= i - 4 < B:
+                finish(i - 4)

@@ -19,7 +19,7 @@ BANK_DT = BF16
 
 FLOPS = 2 * B * J * C * K * C + 2 * B * J * K * J * C
 
-ON_VECTOR = {(0, 0): (2, 3), (0, 1): (2, 3), (1, 0): (3,), (1, 1): (1, 2, 3)}
+ON_VECTOR = {(0, 0): (0, 3), (0, 1): (0, 3), (1, 0): (3,), (1, 1): (1, 2, 3)}
 WARM_UP = 6
 
 
@@ -145,7 +145,10 @@ def tile_block_attention_guide_pb_kernel(tc, g1, res1, adj, spatial_adj, conv2_w
         def turn_bias():
             b_t = bank_tile([P, P], BF16)
             nc.tensor.transpose(b_t[:], b_rows[:], ident_b[:])
-            nc.vector.tensor_copy(out=bias_f[:], in_=b_t[:, 0:16])
+            live["b_t"] = b_t
+
+        def keep_bias():
+            nc.vector.tensor_copy(out=bias_f[:], in_=live["b_t"][:, 0:16])
 
         def stage1(q, j, h):
             bank = bank_tile([P, HALF * J], BANK_DT)
@@ -192,7 +195,7 @@ def tile_block_attention_guide_pb_kernel(tc, g1, res1, adj, spatial_adj, conv2_w
             quantize(h_q, h_s, live[("h_in", b)])
             live[("h_q", b)] = (h_q, h_s)
 
-        def adjacency(h):
+        def weave(h):
             nc.vector.tensor_scalar(
                 out=a_in[h][:].rearrange("p (b w t) -> p b w t", b=HALF, t=4),
                 in0=a_raw[:, HALF * h : HALF * (h + 1)].rearrange("p b t w -> p b w t"),
@@ -200,6 +203,8 @@ def tile_block_attention_guide_pb_kernel(tc, g1, res1, adj, spatial_adj, conv2_w
                 scalar2=None,
                 op0=ALU.mult,
             )
+
+        def adjacency(h):
             quantize(a_q[h], a_s[h], a_in[h])
 
         def stage2(b):
@@ -266,16 +271,17 @@ def tile_block_attention_guide_pb_kernel(tc, g1, res1, adj, spatial_adj, conv2_w
         turn_rows(("g", 0, 1), g_sb[0], perm_f, 1)
         spread(0)
         turn_bias()
-        empty_rows(("g", 0, 0), g_in[0], 0, "S")
-        empty_rows(("g", 0, 1), g_in[0], 1, "V")
+        empty_rows(("g", 0, 0), g_in[0], 0, "V")
+        keep_bias()
+        empty_rows(("g", 0, 1), g_in[0], 1, "S")
         keep_spread(0, gam)
-        quantize(g_q[0], g_s[0], g_in[0])
         turn_rows(("w", 0, 0), w_sb[0], ident_f, 0)
         spread(1)
         turn_rows(("w", 0, 1), w_sb[0], ident_f, 1)
         spin()
-        empty_rows(("w", 0, 0), w_in[0], 0, "S")
-        empty_rows(("w", 0, 1), w_in[0], 1, "V")
+        empty_rows(("w", 0, 0), w_in[0], 0, "V")
+        quantize(g_q[0], g_s[0], g_in[0])
+        empty_rows(("w", 0, 1), w_in[0], 1, "S")
         keep_spread(1, bet)
         quantize(w_q[0], w_s[0], w_in[0])
         for q in range(1, K + 1):
@@ -288,15 +294,12 @@ def tile_block_attention_guide_pb_kernel(tc, g1, res1, adj, spatial_adj, conv2_w
                     spin()
             for j in range(4):
                 stage1(q - 1, j, 0)
-            if q < K:
-                empty_rows(("w", q, 0), w_in[q], 0, "S")
-                empty_rows(("w", q, 1), w_in[q], 1, "V")
-                quantize(w_q[q], w_s[q], w_in[q])
-            else:
-                empty_rows(("g", 1, 0), g_in[1], 0, "S")
-                empty_rows(("g", 1, 1), g_in[1], 1, "V")
-                quantize(g_q[1], g_s[1], g_in[1])
-            for j in range(4):
+            kind, rows, codes, scales, n = ("w", w_in, w_q, w_s, q) if q < K else ("g", g_in, g_q, g_s, 1)
+            empty_rows((kind, n, 0), rows[n], 0, "V")
+            empty_rows((kind, n, 1), rows[n], 1, "S")
+            empty_bank(q - 1, 0, 0)
+            quantize(codes[n], scales[n], rows[n])
+            for j in range(1, 4):
                 empty_bank(q - 1, j, 0)
 
         for i in range(B + 4):
@@ -310,6 +313,8 @@ def tile_block_attention_guide_pb_kernel(tc, g1, res1, adj, spatial_adj, conv2_w
                 for j in range(4):
                     stage1(q, j, 1)
             if i == 0:
+                weave(0)
+                weave(1)
                 adjacency(0)
                 adjacency(1)
             if 0 <= i - 1 < B:

@@ -19,15 +19,32 @@ BANK_DT = BF16
 
 FLOPS = 2 * B * J * C * K * C + 2 * B * J * K * J * C
 
-ON_VECTOR = {(0, 0): (0, 3), (0, 1): (0, 3), (1, 0): (3,), (1, 1): (1, 2, 3)}
+ON_VECTOR = {(0, 0): (0, 3), (0, 1): (0, 3), (1, 0): (2, 3), (1, 1): (0, 1)}
 WARM_UP = 6
+RD = "SSSSSS"
+RH = "SS"
+RD0 = "VVVVVV"
+NB = 1
+LAG = 1
+LATE = ((0, 1), (2,), (3,))
+AQ = (0, 2)
+HB = 4
+AH = 2
+WVP = (-2, -1)
+WVE = "VV"
+SL = ()
+SOFF = (3, 4, 5)
+GB = "pe"
+LOADS = "g0 w0 w1 w2 w3 g1 a0 a1 r0 r1"
+SPINS = (0, 1, 2)
+OFF = (1, 2, 3, 3, 4)
 
 
 def tile_block_attention_guide_pb_kernel(tc, g1, res1, adj, spatial_adj, conv2_w, conv2_b, s2, norm2_g, norm2_b, out_0, out_1):
     nc = tc.nc
     with ExitStack() as ctx:
         keep = ctx.enter_context(tc.tile_pool(name="keep", bufs=1))
-        work = ctx.enter_context(tc.tile_pool(name="work", bufs=3))
+        work = ctx.enter_context(tc.tile_pool(name="work", bufs=HB))
         psum = ctx.enter_context(tc.psum_pool(name="psum", bufs=8))
         ctx.enter_context(tc.manual_schedule())
 
@@ -38,6 +55,7 @@ def tile_block_attention_guide_pb_kernel(tc, g1, res1, adj, spatial_adj, conv2_w
         b_rows = keep.tile([P, P], BF16, name="b_rows")
         gb_rows = keep.tile([P, 2 * C], BF16, name="gb_rows")
         gain = keep.tile([P, 1], BF16, name="gain")
+        gain_f = keep.tile([P, 1], F32, name="gain_f")
         ones = keep.tile([P, P], BF16, name="ones")
         idle = keep.tile([P, C], BF16, name="idle")
         warm = keep.tile([P, 1], F32, name="warm")
@@ -48,6 +66,8 @@ def tile_block_attention_guide_pb_kernel(tc, g1, res1, adj, spatial_adj, conv2_w
         perm_f = keep.tile([P, P], F32, name="perm_f")
         ident_b = keep.tile([P, P], BF16, name="ident_b")
         bias_f = keep.tile([P, 16], F32, name="bias_f")
+        c_rows = keep.tile([P, P], BF16, name="c_rows")
+        cols_f = keep.tile([P, 8], F32, name="cols_f")
         g_in = [keep.tile([P, 4 * C], BF16, name="g_in%d" % h, align_bytes=64) for h in range(2)]
         g_q = [keep.tile([P, C], U32, name="g_q%d" % h, align_bytes=64) for h in range(2)]
         g_s = [keep.tile([P, C], U8, name="g_s%d" % h, align_bytes=64) for h in range(2)]
@@ -66,8 +86,11 @@ def tile_block_attention_guide_pb_kernel(tc, g1, res1, adj, spatial_adj, conv2_w
         nc.vector.memset(b_rows[:], 0.0)
         nc.vector.memset(gain[:], 1.0)
         nc.vector.memset(warm[:], 1.0)
-        nc.scalar.dma_start(out=gb_rows[0:1, 0:C], in_=norm2_g.rearrange("(o c) -> o c", o=1))
-        nc.scalar.dma_start(out=gb_rows[0:1, C : 2 * C], in_=norm2_b.rearrange("(o c) -> o c", o=1))
+        if SL:
+            nc.gpsimd.memset(c_rows[:], 0.0)
+        if GB == "pe":
+            nc.scalar.dma_start(out=gb_rows[0:1, 0:C], in_=norm2_g.rearrange("(o c) -> o c", o=1))
+            nc.scalar.dma_start(out=gb_rows[0:1, C : 2 * C], in_=norm2_b.rearrange("(o c) -> o c", o=1))
         nc.scalar.dma_start(out=b_rows[0:16, :], in_=conv2_b.rearrange("(j p) -> j p", p=P))
         nc.scalar.activation(out=warm2[:], in_=warm[:], func=ACT.Abs_reciprocal_sqrt)
 
@@ -80,25 +103,38 @@ def tile_block_attention_guide_pb_kernel(tc, g1, res1, adj, spatial_adj, conv2_w
                 in_=conv2_w[C * q + P * lo : C * q + P * hi, :].rearrange("(j p) c -> p j c", p=P),
             )
 
-        load_g(0, 0, 2)
-        load_g(0, 2, 4)
-        load_w(0, 0, 2)
-        load_w(0, 2, 4)
-        load_w(1, 0, 4)
-        load_w(2, 0, 4)
-        load_w(3, 0, 4)
-        load_g(1, 0, 4)
-        nc.sync.dma_start(out=gain[0:32, :], in_=s2.partition_broadcast(32))
-        for h in range(2):
+        def load_a(h):
             some = slice(HALF * h, HALF * (h + 1))
             nc.sync.dma_start(
                 out=a_raw[32:128, some].rearrange("p b t w -> p b (t w)"),
                 in_=spatial_adj.rearrange("k (m t) w -> (k m) (t w)", t=4).unsqueeze(1).to_broadcast([96, HALF, 4 * J]),
             )
             nc.sync.dma_start(out=a_raw[0:32, some], in_=adj[some].rearrange("b o (m t) w -> m (b o) t w", t=4))
-        for h in range(2):
-            some = slice(HALF * h, HALF * (h + 1))
-            nc.sync.dma_start(out=res_sb[:, some, :], in_=res1[some].rearrange("b w c -> w b c"))
+
+        for c in LOADS.split():
+            if c == "g0":
+                load_g(0, 0, 2)
+                load_g(0, 2, 4)
+            elif c == "w0":
+                load_w(0, 0, 2)
+                load_w(0, 2, 4)
+            elif c[0] == "w":
+                load_w(int(c[1]), 0, 4)
+            elif c == "g1":
+                load_g(1, 0, 4)
+            elif c[0] == "a":
+                if c == "a0":
+                    nc.sync.dma_start(out=gain[0:32, :], in_=s2.partition_broadcast(32))
+                load_a(int(c[1]))
+            elif c[0] == "r":
+                some = slice(HALF * int(c[1]), HALF * (int(c[1]) + 1))
+                nc.sync.dma_start(out=res_sb[:, some, :], in_=res1[some].rearrange("b w c -> w b c"))
+            elif c == "cr":
+                nc.sync.dma_start(out=c_rows[0:4, :], in_=norm2_g.rearrange("(j p) -> j p", p=P))
+                nc.sync.dma_start(out=c_rows[4:8, :], in_=norm2_b.rearrange("(j p) -> j p", p=P))
+            elif c == "gb":
+                nc.sync.dma_start(out=gam[:], in_=norm2_g.partition_broadcast(P))
+                nc.sync.dma_start(out=bet[:], in_=norm2_b.partition_broadcast(P))
 
         masks.make_identity(nc, ident_f[:])
         nc.vector.tensor_copy(
@@ -187,7 +223,7 @@ def tile_block_attention_guide_pb_kernel(tc, g1, res1, adj, spatial_adj, conv2_w
             if pair == 0:
                 h_in = work.tile([P, 4 * C], BF16, name="h_in", tag="h_in", align_bytes=64)
                 live[("h_in", b)] = h_in
-            empty_rows(("h", b, pair), live[("h_in", b)], pair, "S")
+            empty_rows(("h", b, pair), live[("h_in", b)], pair, RH[pair])
 
         def quantize_h(b):
             h_q = work.tile([P, C], U32, name="h_q", tag="h_q", align_bytes=64)
@@ -195,14 +231,13 @@ def tile_block_attention_guide_pb_kernel(tc, g1, res1, adj, spatial_adj, conv2_w
             quantize(h_q, h_s, live[("h_in", b)])
             live[("h_q", b)] = (h_q, h_s)
 
-        def weave(h):
-            nc.vector.tensor_scalar(
-                out=a_in[h][:].rearrange("p (b w t) -> p b w t", b=HALF, t=4),
-                in0=a_raw[:, HALF * h : HALF * (h + 1)].rearrange("p b t w -> p b w t"),
-                scalar1=gain[:, 0:1],
-                scalar2=None,
-                op0=ALU.mult,
-            )
+        def weave(h, eng):
+            dst = a_in[h][:].rearrange("p (b w t) -> p b w t", b=HALF, t=4)
+            src = a_raw[:, HALF * h : HALF * (h + 1)].rearrange("p b t w -> p b w t")
+            if eng == "V":
+                nc.vector.tensor_scalar(out=dst, in0=src, scalar1=gain[:, 0:1], scalar2=None, op0=ALU.mult)
+            else:
+                nc.scalar.activation(out=dst, in_=src, func=ACT.Copy, scale=gain_f[:, 0:1])
 
         def adjacency(h):
             quantize(a_q[h], a_s[h], a_in[h])
@@ -264,46 +299,98 @@ def tile_block_attention_guide_pb_kernel(tc, g1, res1, adj, spatial_adj, conv2_w
             )
             nc.sync.dma_start(out=out_1[b], in_=xn[:])
 
+        def turn_cols():
+            c_t = bank_tile([P, P], BF16)
+            nc.tensor.transpose(c_t[:], c_rows[:], ident_b[:])
+            nc.scalar.copy(out=cols_f[:], in_=c_t[:, 0:8])
+
+        def norm_rows(b):
+            x2, total, negm = live[("x2", b)]
+            rstd = live[("rstd", b)]
+            nmr = work.tile([P, 1], F32, name="nmr", tag="nmr")
+            nc.scalar.activation(out=nmr[:], in_=negm[:], func=ACT.Copy, scale=rstd[:, 0:1])
+            xh = work.tile([P, C], F32, name="xh", tag="xh")
+            nc.scalar.activation(out=xh[:], in_=x2[:], func=ACT.Identity, bias=nmr[:, 0:1], scale=rstd[:, 0:1])
+            tx = bank_tile([P, 4, P], F32)
+            for j in range(4):
+                nc.tensor.transpose(tx[:, j, :], xh[:, P * j : P * (j + 1)], ident_f[:])
+            live[("tx", b)] = tx
+
+        def gain_cols(b):
+            y_t = work.tile([P, 4, P], F32, name="y_t", tag="y_t")
+            for j in range(4):
+                nc.scalar.activation(
+                    out=y_t[:, j, :], in_=live[("tx", b)][:, j, :], func=ACT.Identity,
+                    bias=cols_f[:, 4 + j : 5 + j], scale=cols_f[:, j : j + 1],
+                )
+            ty = bank_tile([P, 4, P], F32)
+            for j in range(4):
+                nc.tensor.transpose(ty[:, j, :], y_t[:, j, :], ident_f[:])
+            live[("ty", b)] = ty
+
+        def keep_norm(b):
+            xn = work.tile([P, C], F32, name="xn", tag="xn")
+            nc.scalar.copy(out=xn[:], in_=live[("ty", b)][:].rearrange("p j c -> p (j c)"))
+            nc.sync.dma_start(out=out_1[b], in_=xn[:])
+
         for i in range(WARM_UP):
             spin()
 
-        turn_rows(("g", 0, 0), g_sb[0], perm_f, 0)
-        turn_rows(("g", 0, 1), g_sb[0], perm_f, 1)
-        spread(0)
-        turn_bias()
-        empty_rows(("g", 0, 0), g_in[0], 0, "V")
-        keep_bias()
-        empty_rows(("g", 0, 1), g_in[0], 1, "S")
-        keep_spread(0, gam)
-        turn_rows(("w", 0, 0), w_sb[0], ident_f, 0)
-        spread(1)
-        turn_rows(("w", 0, 1), w_sb[0], ident_f, 1)
-        spin()
-        empty_rows(("w", 0, 0), w_in[0], 0, "V")
-        quantize(g_q[0], g_s[0], g_in[0])
-        empty_rows(("w", 0, 1), w_in[0], 1, "S")
-        keep_spread(1, bet)
-        quantize(w_q[0], w_s[0], w_in[0])
-        for q in range(1, K + 1):
-            for pair in range(2):
-                if q < K:
-                    turn_rows(("w", q, pair), w_sb[q], ident_f, pair)
-                else:
-                    turn_rows(("g", 1, pair), g_sb[1], perm_f, pair)
-                if q == 1:
+        seq = [("g", 0), ("w", 0), ("w", 1), ("w", 2), ("w", 3), ("g", 1)]
+        src = {"g": g_sb, "w": w_sb}
+        mat = {"g": perm_f, "w": ident_f}
+        dst = {"g": (g_in, g_q, g_s), "w": (w_in, w_q, w_s)}
+        for i in range(len(seq) + AH):
+            if i < len(seq):
+                kind, n = seq[i]
+                for pair in range(2):
+                    turn_rows((kind, n, pair), src[kind][n], mat[kind], pair)
+                    if GB == "pe" and i == 1 and pair == 0:
+                        spread(1)
+                    if i < len(SPINS) and SPINS[i] == 2:
+                        spin()
+                if i == 0:
+                    if GB == "pe":
+                        spread(0)
+                    turn_bias()
+                for x in range(SPINS[i] if i < len(SPINS) and SPINS[i] != 2 else 0):
                     spin()
-            for j in range(4):
-                stage1(q - 1, j, 0)
-            kind, rows, codes, scales, n = ("w", w_in, w_q, w_s, q) if q < K else ("g", g_in, g_q, g_s, 1)
-            empty_rows((kind, n, 0), rows[n], 0, "V")
-            empty_rows((kind, n, 1), rows[n], 1, "S")
-            empty_bank(q - 1, 0, 0)
-            quantize(codes[n], scales[n], rows[n])
-            for j in range(1, 4):
-                empty_bank(q - 1, j, 0)
+            q = i - 1 - AH
+            if 0 <= q < K:
+                for j in range(4):
+                    stage1(q, j, 0)
+            vfirst = [j for j in range(4) if 0 <= q < K and j in ON_VECTOR[(0, q % 2)]][:NB]
+            if i < len(seq):
+                grouped, codes, scales = dst[kind]
+                empty_rows((kind, n, 0), grouped[n], 0, RD0[i])
+                if i == 0:
+                    keep_bias()
+                empty_rows((kind, n, 1), grouped[n], 1, RD[i])
+                if GB == "pe" and i < 2:
+                    keep_spread(i, (gam, bet)[i])
+                if i == 1 and LAG:
+                    quantize(g_q[0], g_s[0], g_in[0])
+                for j in vfirst:
+                    empty_bank(q, j, 0)
+                if not (i == 0 and LAG):
+                    quantize(codes[n], scales[n], grouped[n])
+            if 0 <= q < K:
+                for j in range(4):
+                    if i >= len(seq) or j not in vfirst:
+                        empty_bank(q, j, 0)
+            for h in range(2):
+                if WVP[h] == i - len(seq) - AH:
+                    if WVE[h] == "S":
+                        nc.vector.tensor_copy(out=gain_f[:], in_=gain[:])
+                    weave(h, WVE[h])
+            for h in range(2):
+                if AQ[h] == i - len(seq) - AH:
+                    adjacency(h)
 
-        for i in range(B + 4):
-            late = (2 * i, 2 * i + 1) if i < 2 else ()
+        for i in range(B + max(max(OFF), SOFF[2] if SL else 0)):
+            late = LATE[i] if i < len(LATE) else ()
+            if SL and i == 3:
+                turn_cols()
             if i < B:
                 for pair in range(2):
                     turn_h(i, pair)
@@ -312,22 +399,31 @@ def tile_block_attention_guide_pb_kernel(tc, g1, res1, adj, spatial_adj, conv2_w
             for q in late:
                 for j in range(4):
                     stage1(q, j, 1)
-            if i == 0:
-                weave(0)
-                weave(1)
-                adjacency(0)
-                adjacency(1)
-            if 0 <= i - 1 < B:
-                quantize_h(i - 1)
-                stage2(i - 1)
-            if 0 <= i - 3 < B:
-                spread_of(i - 3)
+            for h in range(2):
+                if WVP[h] == i:
+                    if WVE[h] == "S":
+                        nc.vector.tensor_copy(out=gain_f[:], in_=gain[:])
+                    weave(h, WVE[h])
+            for h in range(2):
+                if AQ[h] == i:
+                    adjacency(h)
+            if 0 <= i - OFF[0] < B:
+                quantize_h(i - OFF[0])
+                stage2(i - OFF[0])
+            if i - SOFF[2] in SL:
+                keep_norm(i - SOFF[2])
+            if i - SOFF[1] in SL:
+                gain_cols(i - SOFF[1])
+            if 0 <= i - OFF[2] < B:
+                spread_of(i - OFF[2])
+            if i - SOFF[0] in SL:
+                norm_rows(i - SOFF[0])
             for q in late:
                 for j in range(4):
                     empty_bank(q, j, 1)
-            if 0 <= i - 2 < B:
-                residual(i - 2)
-            if 0 <= i - 3 < B:
-                centre(i - 3)
-            if 0 <= i - 4 < B:
-                finish(i - 4)
+            if 0 <= i - OFF[1] < B:
+                residual(i - OFF[1])
+            if 0 <= i - OFF[3] < B and i - OFF[3] not in SL:
+                centre(i - OFF[3])
+            if 0 <= i - OFF[4] < B and i - OFF[4] not in SL:
+                finish(i - OFF[4])

@@ -29,6 +29,8 @@ LAG = 1
 LATE = ((0, 1), (2,), (3,))
 AQ = (0, 2)
 HB = 4
+LNB = 4
+ROW2 = 1
 AH = 2
 WVP = (-2, -1)
 WVE = "VV"
@@ -45,6 +47,7 @@ def tile_block_attention_guide_pb_kernel(tc, g1, res1, adj, spatial_adj, conv2_w
     with ExitStack() as ctx:
         keep = ctx.enter_context(tc.tile_pool(name="keep", bufs=1))
         work = ctx.enter_context(tc.tile_pool(name="work", bufs=HB))
+        lnp = ctx.enter_context(tc.tile_pool(name="lnp", bufs=LNB))
         psum = ctx.enter_context(tc.psum_pool(name="psum", bufs=8))
         ctx.enter_context(tc.manual_schedule())
 
@@ -52,7 +55,8 @@ def tile_block_attention_guide_pb_kernel(tc, g1, res1, adj, spatial_adj, conv2_w
         w_sb = [keep.tile([P, 4, C], BF16, name="w_sb%d" % q) for q in range(K)]
         a_raw = keep.tile([P, B, 4, J], BF16, name="a_raw")
         res_sb = keep.tile([P, B, C], BF16, name="res_sb")
-        b_rows = keep.tile([P, P], BF16, name="b_rows")
+        b_rows = keep.tile([P, P], F32 if ROW2 else BF16, name="b_rows")
+        bias_w = keep.tile([P, 8], F32, name="bias_w")
         gb_rows = keep.tile([P, 2 * C], BF16, name="gb_rows")
         gain = keep.tile([P, 1], BF16, name="gain")
         gain_f = keep.tile([P, 1], F32, name="gain_f")
@@ -91,13 +95,28 @@ def tile_block_attention_guide_pb_kernel(tc, g1, res1, adj, spatial_adj, conv2_w
         if GB == "pe":
             nc.scalar.dma_start(out=gb_rows[0:1, 0:C], in_=norm2_g.rearrange("(o c) -> o c", o=1))
             nc.scalar.dma_start(out=gb_rows[0:1, C : 2 * C], in_=norm2_b.rearrange("(o c) -> o c", o=1))
-        nc.scalar.dma_start(out=b_rows[0:16, :], in_=conv2_b.rearrange("(j p) -> j p", p=P))
+        if ROW2:
+            nc.scalar.dma_start(out=b_rows[0:8, :].bitcast(BF16), in_=conv2_b.rearrange("(r x) -> r x", x=2 * P))
+        else:
+            nc.scalar.dma_start(out=b_rows[0:16, :], in_=conv2_b.rearrange("(j p) -> j p", p=P))
         nc.scalar.activation(out=warm2[:], in_=warm[:], func=ACT.Abs_reciprocal_sqrt)
 
         def load_g(h, lo, hi):
-            nc.sync.dma_start(out=g_sb[h][:, lo:hi, :], in_=g1[HALF * h + lo : HALF * h + hi].rearrange("b v c -> v b c"))
+            if ROW2:
+                nc.sync.dma_start(
+                    out=g_sb[h][:, lo:hi, :].rearrange("p (d i) c -> p d (i c)", i=2),
+                    in_=g1[HALF * h + lo : HALF * h + hi].rearrange("b v c -> (b v) c").rearrange("(d p i) c -> p d (i c)", p=P, i=2),
+                )
+            else:
+                nc.sync.dma_start(out=g_sb[h][:, lo:hi, :], in_=g1[HALF * h + lo : HALF * h + hi].rearrange("b v c -> v b c"))
 
         def load_w(q, lo, hi):
+            if ROW2:
+                nc.sync.dma_start(
+                    out=w_sb[q][:, lo:hi, :].rearrange("p (d i) c -> p d (i c)", i=2),
+                    in_=conv2_w[C * q + P * lo : C * q + P * hi, :].rearrange("(d p i) c -> p d (i c)", p=P, i=2),
+                )
+                return
             nc.sync.dma_start(
                 out=w_sb[q][:, lo:hi, :],
                 in_=conv2_w[C * q + P * lo : C * q + P * hi, :].rearrange("(j p) c -> p j c", p=P),
@@ -137,10 +156,16 @@ def tile_block_attention_guide_pb_kernel(tc, g1, res1, adj, spatial_adj, conv2_w
                 nc.sync.dma_start(out=bet[:], in_=norm2_b.partition_broadcast(P))
 
         masks.make_identity(nc, ident_f[:])
-        nc.vector.tensor_copy(
-            out=perm_f[:].rearrange("p (u m e) -> p u m e", u=2, e=2),
-            in_=ident_f[:].rearrange("p (m u e) -> p u m e", u=2, e=2),
-        )
+        if ROW2:
+            nc.vector.tensor_copy(
+                out=perm_f[:].rearrange("p (d u m) -> p d u m", d=2, u=2),
+                in_=ident_f[:].rearrange("p (d m u) -> p d u m", d=2, u=2),
+            )
+        else:
+            nc.vector.tensor_copy(
+                out=perm_f[:].rearrange("p (u m e) -> p u m e", u=2, e=2),
+                in_=ident_f[:].rearrange("p (m u e) -> p u m e", u=2, e=2),
+            )
         nc.vector.tensor_copy(out=ident_b[:], in_=ident_f[:])
 
         def bank_tile(shape, dtype):
@@ -172,6 +197,10 @@ def tile_block_attention_guide_pb_kernel(tc, g1, res1, adj, spatial_adj, conv2_w
             live[key] = tr
 
         def empty_rows(key, grouped, pair, eng):
+            if ROW2 and key[0] != "w":
+                dst = grouped[:].bitcast(F32).rearrange("p (d r a u) -> p d r a u", d=2, a=2, u=2)
+                copy_words(eng, dst[:, pair], live[key][:].rearrange("p a u r -> p r a u"))
+                return
             dst = grouped[:].bitcast(F32).rearrange("p (a r u) -> p a r u", a=4, u=2)
             copy_words(eng, dst[:, 2 * pair : 2 * pair + 2], live[key][:].rearrange("p a u r -> p a r u"))
 
@@ -179,12 +208,15 @@ def tile_block_attention_guide_pb_kernel(tc, g1, res1, adj, spatial_adj, conv2_w
             nc.vector.quantize_mx(out=codes[:].bitcast(FP8X4), scales=scales[:], in_=grouped[:])
 
         def turn_bias():
-            b_t = bank_tile([P, P], BF16)
-            nc.tensor.transpose(b_t[:], b_rows[:], ident_b[:])
+            b_t = bank_tile([P, P], F32 if ROW2 else BF16)
+            nc.tensor.transpose(b_t[:], b_rows[:], ident_f[:] if ROW2 else ident_b[:])
             live["b_t"] = b_t
 
         def keep_bias():
-            nc.vector.tensor_copy(out=bias_f[:], in_=live["b_t"][:, 0:16])
+            if ROW2:
+                nc.vector.tensor_copy(out=bias_w[:], in_=live["b_t"][:, 0:8])
+            else:
+                nc.vector.tensor_copy(out=bias_f[:], in_=live["b_t"][:, 0:16])
 
         def stage1(q, j, h):
             bank = bank_tile([P, HALF * J], BANK_DT)
@@ -204,7 +236,7 @@ def tile_block_attention_guide_pb_kernel(tc, g1, res1, adj, spatial_adj, conv2_w
             bank = live[("bank", q, j, h)]
             dst = h_t[h][j][:].rearrange("p (b u k x) -> p b u k x", b=HALF, u=2, k=K)[:, :, :, q, :]
             src = bank[:].rearrange("p (b u x) -> p b u x", b=HALF, u=2)
-            col = bias_f[:, 4 * q + j : 4 * q + j + 1]
+            col = (bias_w[:].bitcast(BF16) if ROW2 else bias_f)[:, 4 * q + j : 4 * q + j + 1]
             if j in ON_VECTOR[(h, q % 2)]:
                 nc.vector.tensor_scalar(out=dst, in0=src, scalar1=col, scalar2=None, op0=ALU.add)
             else:
@@ -259,25 +291,25 @@ def tile_block_attention_guide_pb_kernel(tc, g1, res1, adj, spatial_adj, conv2_w
             live[("acc", b)] = acc
 
         def residual(b):
-            x2 = work.tile([P, C], F32, name="x2", tag="x2")
-            total = work.tile([P, 1], F32, name="total", tag="total")
+            x2 = lnp.tile([P, C], F32, name="x2", tag="x2")
+            total = lnp.tile([P, 1], F32, name="total", tag="total")
             nc.vector.scalar_tensor_tensor(
                 out=x2[:], in0=live[("acc", b)][:], scalar=1.0, in1=res_sb[:, b, :],
                 op0=ALU.mult, op1=ALU.add, accum_out=total[:],
             )
             nc.sync.dma_start(out=out_0[b], in_=x2[:])
-            negm = work.tile([P, 1], F32, name="negm", tag="negm")
+            negm = lnp.tile([P, 1], F32, name="negm", tag="negm")
             nc.scalar.activation(out=negm[:], in_=total[:], func=ACT.Copy, scale=-1.0 / C)
             live[("x2", b)] = (x2, total, negm)
 
         def spread_of(b):
             x2, total, negm = live[("x2", b)]
-            junk = work.tile([P, C], BF16, name="junk", tag="junk")
-            ssq = work.tile([P, 1], F32, name="ssq", tag="ssq")
+            junk = lnp.tile([P, C], BF16, name="junk", tag="junk")
+            ssq = lnp.tile([P, 1], F32, name="ssq", tag="ssq")
             nc.scalar.activation(
                 out=junk[:], in_=x2[:], func=ACT.Square, bias=total[:, 0:1], scale=-1.0 * C, accum_out=ssq[:]
             )
-            rstd = work.tile([P, 1], F32, name="rstd", tag="rstd")
+            rstd = lnp.tile([P, 1], F32, name="rstd", tag="rstd")
             nc.scalar.activation(
                 out=rstd[:], in_=ssq[:], func=ACT.Abs_reciprocal_sqrt, bias=EPS, scale=1.0 / (C * C * C)
             )
@@ -285,14 +317,14 @@ def tile_block_attention_guide_pb_kernel(tc, g1, res1, adj, spatial_adj, conv2_w
 
         def centre(b):
             x2, total, negm = live[("x2", b)]
-            cen = work.tile([P, C], F32, name="cen", tag="cen")
+            cen = lnp.tile([P, C], F32, name="cen", tag="cen")
             nc.vector.scalar_tensor_tensor(
                 out=cen[:], in0=x2[:], scalar=negm[:, 0:1], in1=gam[:], op0=ALU.add, op1=ALU.mult
             )
             live[("cen", b)] = cen
 
         def finish(b):
-            xn = work.tile([P, C], F32, name="xn", tag="xn")
+            xn = lnp.tile([P, C], F32, name="xn", tag="xn")
             nc.vector.scalar_tensor_tensor(
                 out=xn[:], in0=live[("cen", b)][:], scalar=live[("rstd", b)][:, 0:1], in1=bet[:],
                 op0=ALU.mult, op1=ALU.add,
@@ -329,7 +361,7 @@ def tile_block_attention_guide_pb_kernel(tc, g1, res1, adj, spatial_adj, conv2_w
             live[("ty", b)] = ty
 
         def keep_norm(b):
-            xn = work.tile([P, C], F32, name="xn", tag="xn")
+            xn = lnp.tile([P, C], F32, name="xn", tag="xn")
             nc.scalar.copy(out=xn[:], in_=live[("ty", b)][:].rearrange("p j c -> p (j c)"))
             nc.sync.dma_start(out=out_1[b], in_=xn[:])
 

@@ -31,6 +31,7 @@ AQ = (0, 2)
 HB = 4
 LNB = 4
 ROW2 = 1
+SQ1 = 0
 AH = 2
 WVP = (-2, -1)
 WVE = "VV"
@@ -38,7 +39,7 @@ SL = ()
 SOFF = (3, 4, 5)
 GB = "pe"
 LOADS = "g0 w0 w1 w2 w3 g1 a0 a1 r0 r1"
-SPINS = (0, 1, 2)
+SPINS = (0, 0, 0)
 OFF = (1, 2, 3, 3, 4)
 
 
@@ -309,9 +310,12 @@ def tile_block_attention_guide_pb_kernel(tc, g1, res1, adj, spatial_adj, conv2_w
             nc.scalar.activation(
                 out=junk[:], in_=x2[:], func=ACT.Square, bias=total[:, 0:1], scale=-1.0 * C, accum_out=ssq[:]
             )
+            live[("ssq", b)] = ssq
+
+        def rstd_of(b):
             rstd = lnp.tile([P, 1], F32, name="rstd", tag="rstd")
             nc.scalar.activation(
-                out=rstd[:], in_=ssq[:], func=ACT.Abs_reciprocal_sqrt, bias=EPS, scale=1.0 / (C * C * C)
+                out=rstd[:], in_=live[("ssq", b)][:], func=ACT.Abs_reciprocal_sqrt, bias=EPS, scale=1.0 / (C * C * C)
             )
             live[("rstd", b)] = rstd
 
@@ -423,11 +427,15 @@ def tile_block_attention_guide_pb_kernel(tc, g1, res1, adj, spatial_adj, conv2_w
             late = LATE[i] if i < len(LATE) else ()
             if SL and i == 3:
                 turn_cols()
+            if SQ1 and 0 <= i - OFF[2] < B:
+                spread_of(i - OFF[2])
             if i < B:
                 for pair in range(2):
                     turn_h(i, pair)
                 for pair in range(2):
                     empty_h(i, pair)
+            if SQ1 and 0 <= i - OFF[2] < B:
+                rstd_of(i - OFF[2])
             for q in late:
                 for j in range(4):
                     stage1(q, j, 1)
@@ -446,8 +454,9 @@ def tile_block_attention_guide_pb_kernel(tc, g1, res1, adj, spatial_adj, conv2_w
                 keep_norm(i - SOFF[2])
             if i - SOFF[1] in SL:
                 gain_cols(i - SOFF[1])
-            if 0 <= i - OFF[2] < B:
+            if not SQ1 and 0 <= i - OFF[2] < B:
                 spread_of(i - OFF[2])
+                rstd_of(i - OFF[2])
             if i - SOFF[0] in SL:
                 norm_rows(i - SOFF[0])
             for q in late:

@@ -19,7 +19,7 @@ BANK_DT = BF16
 
 FLOPS = 2 * B * J * C * K * C + 2 * B * J * K * J * C
 
-ON_VECTOR = {(0, 0): (0, 3), (0, 1): (0, 3), (1, 0): (2, 3), (1, 1): (0, 1)}
+ON_VECTOR = {(0, 0): (0, 3), (0, 1): (0, 3), (1, 0): (1, 2, 3), (1, 1): (0, 1)}
 WARM_UP = 6
 RD = "SSSSSS"
 RH = "SS"
@@ -32,6 +32,13 @@ HB = 4
 LNB = 4
 ROW2 = 1
 SQ1 = 0
+TAIL = 2
+WS = (2, 2, 2, 2, 2)
+EGB = 0
+RHR = ()
+SLAST = 0
+SQ2 = 1
+GNEG = 0
 AH = 2
 WVP = (-2, -1)
 WVE = "VV"
@@ -85,10 +92,14 @@ def tile_block_attention_guide_pb_kernel(tc, g1, res1, adj, spatial_adj, conv2_w
         h_t = [[keep.tile([P, HALF * C], BF16, name="h_t%d_%d" % (h, j)) for j in range(4)] for h in range(2)]
         live = {}
 
+        if EGB:
+            nc.vector.memset(gb_rows[:], 0.0)
+            nc.vector.memset(b_rows[:], 0.0)
         nc.vector.memset(ones[:], 1.0)
         nc.vector.memset(idle[:], 0.0)
-        nc.vector.memset(gb_rows[:], 0.0)
-        nc.vector.memset(b_rows[:], 0.0)
+        if not EGB:
+            nc.vector.memset(gb_rows[:], 0.0)
+            nc.vector.memset(b_rows[:], 0.0)
         nc.vector.memset(gain[:], 1.0)
         nc.vector.memset(warm[:], 1.0)
         if SL:
@@ -135,13 +146,12 @@ def tile_block_attention_guide_pb_kernel(tc, g1, res1, adj, spatial_adj, conv2_w
             if c == "g0":
                 load_g(0, 0, 2)
                 load_g(0, 2, 4)
-            elif c == "w0":
-                load_w(0, 0, 2)
-                load_w(0, 2, 4)
             elif c[0] == "w":
-                load_w(int(c[1]), 0, 4)
+                for x in range(WS[int(c[1])]):
+                    load_w(int(c[1]), 4 * x // WS[int(c[1])], 4 * (x + 1) // WS[int(c[1])])
             elif c == "g1":
-                load_g(1, 0, 4)
+                for x in range(WS[4]):
+                    load_g(1, 4 * x // WS[4], 4 * (x + 1) // WS[4])
             elif c[0] == "a":
                 if c == "a0":
                     nc.sync.dma_start(out=gain[0:32, :], in_=s2.partition_broadcast(32))
@@ -256,7 +266,7 @@ def tile_block_attention_guide_pb_kernel(tc, g1, res1, adj, spatial_adj, conv2_w
             if pair == 0:
                 h_in = work.tile([P, 4 * C], BF16, name="h_in", tag="h_in", align_bytes=64)
                 live[("h_in", b)] = h_in
-            empty_rows(("h", b, pair), live[("h_in", b)], pair, RH[pair])
+            empty_rows(("h", b, pair), live[("h_in", b)], pair, (RHR[b] if b < len(RHR) else RH)[pair])
 
         def quantize_h(b):
             h_q = work.tile([P, C], U32, name="h_q", tag="h_q", align_bytes=64)
@@ -300,7 +310,10 @@ def tile_block_attention_guide_pb_kernel(tc, g1, res1, adj, spatial_adj, conv2_w
             )
             nc.sync.dma_start(out=out_0[b], in_=x2[:])
             negm = lnp.tile([P, 1], F32, name="negm", tag="negm")
-            nc.scalar.activation(out=negm[:], in_=total[:], func=ACT.Copy, scale=-1.0 / C)
+            if GNEG:
+                nc.gpsimd.tensor_scalar(out=negm[:], in0=total[:], scalar1=-1.0 / C, scalar2=0.0, op0=ALU.mult, op1=ALU.add)
+            else:
+                nc.scalar.activation(out=negm[:], in_=total[:], func=ACT.Copy, scale=-1.0 / C)
             live[("x2", b)] = (x2, total, negm)
 
         def spread_of(b):
@@ -329,11 +342,14 @@ def tile_block_attention_guide_pb_kernel(tc, g1, res1, adj, spatial_adj, conv2_w
 
         def finish(b):
             xn = lnp.tile([P, C], F32, name="xn", tag="xn")
-            nc.vector.scalar_tensor_tensor(
-                out=xn[:], in0=live[("cen", b)][:], scalar=live[("rstd", b)][:, 0:1], in1=bet[:],
-                op0=ALU.mult, op1=ALU.add,
-            )
-            nc.sync.dma_start(out=out_1[b], in_=xn[:])
+            parts = TAIL if b == B - 1 else 1
+            for x in range(parts):
+                cols = slice(C * x // parts, C * (x + 1) // parts)
+                nc.vector.scalar_tensor_tensor(
+                    out=xn[:, cols], in0=live[("cen", b)][:, cols], scalar=live[("rstd", b)][:, 0:1], in1=bet[:, cols],
+                    op0=ALU.mult, op1=ALU.add,
+                )
+                nc.sync.dma_start(out=out_1[b][:, cols], in_=xn[:, cols])
 
         def turn_cols():
             c_t = bank_tile([P, P], BF16)
@@ -371,6 +387,13 @@ def tile_block_attention_guide_pb_kernel(tc, g1, res1, adj, spatial_adj, conv2_w
 
         for i in range(WARM_UP):
             spin()
+        if EGB:
+            spread(0)
+            spread(1)
+            turn_bias()
+            keep_spread(0, gam)
+            keep_spread(1, bet)
+            keep_bias()
 
         seq = [("g", 0), ("w", 0), ("w", 1), ("w", 2), ("w", 3), ("g", 1)]
         src = {"g": g_sb, "w": w_sb}
@@ -381,11 +404,11 @@ def tile_block_attention_guide_pb_kernel(tc, g1, res1, adj, spatial_adj, conv2_w
                 kind, n = seq[i]
                 for pair in range(2):
                     turn_rows((kind, n, pair), src[kind][n], mat[kind], pair)
-                    if GB == "pe" and i == 1 and pair == 0:
+                    if GB == "pe" and i == 1 and pair == 0 and not EGB:
                         spread(1)
                     if i < len(SPINS) and SPINS[i] == 2:
                         spin()
-                if i == 0:
+                if i == 0 and not EGB:
                     if GB == "pe":
                         spread(0)
                     turn_bias()
@@ -399,10 +422,10 @@ def tile_block_attention_guide_pb_kernel(tc, g1, res1, adj, spatial_adj, conv2_w
             if i < len(seq):
                 grouped, codes, scales = dst[kind]
                 empty_rows((kind, n, 0), grouped[n], 0, RD0[i])
-                if i == 0:
+                if i == 0 and not EGB:
                     keep_bias()
                 empty_rows((kind, n, 1), grouped[n], 1, RD[i])
-                if GB == "pe" and i < 2:
+                if GB == "pe" and i < 2 and not EGB:
                     keep_spread(i, (gam, bet)[i])
                 if i == 1 and LAG:
                     quantize(g_q[0], g_s[0], g_in[0])
@@ -450,21 +473,30 @@ def tile_block_attention_guide_pb_kernel(tc, g1, res1, adj, spatial_adj, conv2_w
             if 0 <= i - OFF[0] < B:
                 quantize_h(i - OFF[0])
                 stage2(i - OFF[0])
-            if i - SOFF[2] in SL:
+            if not SLAST and i - SOFF[2] in SL:
                 keep_norm(i - SOFF[2])
-            if i - SOFF[1] in SL:
+            if not SLAST and i - SOFF[1] in SL:
                 gain_cols(i - SOFF[1])
             if not SQ1 and 0 <= i - OFF[2] < B:
                 spread_of(i - OFF[2])
-                rstd_of(i - OFF[2])
-            if i - SOFF[0] in SL:
+                if not SQ2:
+                    rstd_of(i - OFF[2])
+            if not SLAST and i - SOFF[0] in SL:
                 norm_rows(i - SOFF[0])
             for q in late:
                 for j in range(4):
                     empty_bank(q, j, 1)
             if 0 <= i - OFF[1] < B:
                 residual(i - OFF[1])
+            if SQ2 and 0 <= i - OFF[2] < B:
+                rstd_of(i - OFF[2])
             if 0 <= i - OFF[3] < B and i - OFF[3] not in SL:
                 centre(i - OFF[3])
             if 0 <= i - OFF[4] < B and i - OFF[4] not in SL:
                 finish(i - OFF[4])
+            if SLAST and i - SOFF[2] in SL:
+                keep_norm(i - SOFF[2])
+            if SLAST and i - SOFF[1] in SL:
+                gain_cols(i - SOFF[1])
+            if SLAST and i - SOFF[0] in SL:
+                norm_rows(i - SOFF[0])

@@ -15,59 +15,36 @@ B, J, C, K = 8, 128, 512, 4
 EPS = 1e-5
 P = 128
 HALF = 4
-BANK_DT = BF16
+CHUNKS = 4
 
 FLOPS = 2 * B * J * C * K * C + 2 * B * J * K * J * C
 
 ON_VECTOR = {(0, 0): (0, 3), (0, 1): (0, 3), (1, 0): (1, 2, 3), (1, 1): (0, 1)}
 WARM_UP = 6
-RD = "SSSSSS"
-RH = "SS"
-RD0 = "VVVVVV"
-NB = 1
-LAG = 1
-LATE = ((0, 1), (2,), (3,))
-AQ = (0, 2)
-HB = 4
-LNB = 4
-ROW2 = 1
-SQ1 = 0
-TAIL = 2
-WS = (2, 2, 2, 2, 2)
-EGB = 0
-RHR = ()
-SLAST = 0
-SQ2 = 1
-GNEG = 0
-AH = 2
-WVP = (-2, -1)
-WVE = "VV"
-SL = ()
-SOFF = (3, 4, 5)
-GB = "pe"
-LOADS = "g0 w0 w1 w2 w3 g1 a0 a1 r0 r1"
-SPINS = (0, 0, 0)
-OFF = (1, 2, 3, 3, 4)
+LEAD = 2
+LATE_SLICES = ((0, 1), (2,), (3,))
+ADJ_ROUND = (0, 2)
+QUANTISE_LAG, RESIDUAL_LAG, STATS_LAG, CENTRE_LAG, FINISH_LAG = 1, 2, 3, 3, 4
+ROUND_BUFS = 4
+LAST_PIECES = 2
 
 
 def tile_block_attention_guide_pb_kernel(tc, g1, res1, adj, spatial_adj, conv2_w, conv2_b, s2, norm2_g, norm2_b, out_0, out_1):
     nc = tc.nc
     with ExitStack() as ctx:
         keep = ctx.enter_context(tc.tile_pool(name="keep", bufs=1))
-        work = ctx.enter_context(tc.tile_pool(name="work", bufs=HB))
-        lnp = ctx.enter_context(tc.tile_pool(name="lnp", bufs=LNB))
+        work = ctx.enter_context(tc.tile_pool(name="work", bufs=ROUND_BUFS))
         psum = ctx.enter_context(tc.psum_pool(name="psum", bufs=8))
         ctx.enter_context(tc.manual_schedule())
 
         g_sb = [keep.tile([P, HALF, C], BF16, name="g_sb%d" % h) for h in range(2)]
-        w_sb = [keep.tile([P, 4, C], BF16, name="w_sb%d" % q) for q in range(K)]
+        w_sb = [keep.tile([P, CHUNKS, C], BF16, name="w_sb%d" % q) for q in range(K)]
         a_raw = keep.tile([P, B, 4, J], BF16, name="a_raw")
         res_sb = keep.tile([P, B, C], BF16, name="res_sb")
-        b_rows = keep.tile([P, P], F32 if ROW2 else BF16, name="b_rows")
-        bias_w = keep.tile([P, 8], F32, name="bias_w")
+        b_rows = keep.tile([P, P], F32, name="b_rows")
+        bias_w = keep.tile([P, 2 * K], F32, name="bias_w")
         gb_rows = keep.tile([P, 2 * C], BF16, name="gb_rows")
         gain = keep.tile([P, 1], BF16, name="gain")
-        gain_f = keep.tile([P, 1], F32, name="gain_f")
         ones = keep.tile([P, P], BF16, name="ones")
         idle = keep.tile([P, C], BF16, name="idle")
         warm = keep.tile([P, 1], F32, name="warm")
@@ -76,10 +53,6 @@ def tile_block_attention_guide_pb_kernel(tc, g1, res1, adj, spatial_adj, conv2_w
         bet = keep.tile([P, C], BF16, name="bet")
         ident_f = keep.tile([P, P], F32, name="ident_f")
         perm_f = keep.tile([P, P], F32, name="perm_f")
-        ident_b = keep.tile([P, P], BF16, name="ident_b")
-        bias_f = keep.tile([P, 16], F32, name="bias_f")
-        c_rows = keep.tile([P, P], BF16, name="c_rows")
-        cols_f = keep.tile([P, 8], F32, name="cols_f")
         g_in = [keep.tile([P, 4 * C], BF16, name="g_in%d" % h, align_bytes=64) for h in range(2)]
         g_q = [keep.tile([P, C], U32, name="g_q%d" % h, align_bytes=64) for h in range(2)]
         g_s = [keep.tile([P, C], U8, name="g_s%d" % h, align_bytes=64) for h in range(2)]
@@ -89,52 +62,37 @@ def tile_block_attention_guide_pb_kernel(tc, g1, res1, adj, spatial_adj, conv2_w
         a_in = [keep.tile([P, HALF * J * 4], BF16, name="a_in%d" % h, align_bytes=64) for h in range(2)]
         a_q = [keep.tile([P, HALF * J], U32, name="a_q%d" % h, align_bytes=64) for h in range(2)]
         a_s = [keep.tile([P, HALF * J], U8, name="a_s%d" % h, align_bytes=64) for h in range(2)]
-        h_t = [[keep.tile([P, HALF * C], BF16, name="h_t%d_%d" % (h, j)) for j in range(4)] for h in range(2)]
+        h_t = [[keep.tile([P, HALF * C], BF16, name="h_t%d_%d" % (h, j)) for j in range(CHUNKS)] for h in range(2)]
         live = {}
 
-        if EGB:
-            nc.vector.memset(gb_rows[:], 0.0)
-            nc.vector.memset(b_rows[:], 0.0)
         nc.vector.memset(ones[:], 1.0)
         nc.vector.memset(idle[:], 0.0)
-        if not EGB:
-            nc.vector.memset(gb_rows[:], 0.0)
-            nc.vector.memset(b_rows[:], 0.0)
+        nc.vector.memset(gb_rows[:], 0.0)
+        nc.vector.memset(b_rows[:], 0.0)
         nc.vector.memset(gain[:], 1.0)
         nc.vector.memset(warm[:], 1.0)
-        if SL:
-            nc.gpsimd.memset(c_rows[:], 0.0)
-        if GB == "pe":
-            nc.scalar.dma_start(out=gb_rows[0:1, 0:C], in_=norm2_g.rearrange("(o c) -> o c", o=1))
-            nc.scalar.dma_start(out=gb_rows[0:1, C : 2 * C], in_=norm2_b.rearrange("(o c) -> o c", o=1))
-        if ROW2:
-            nc.scalar.dma_start(out=b_rows[0:8, :].bitcast(BF16), in_=conv2_b.rearrange("(r x) -> r x", x=2 * P))
-        else:
-            nc.scalar.dma_start(out=b_rows[0:16, :], in_=conv2_b.rearrange("(j p) -> j p", p=P))
+        nc.scalar.dma_start(out=gb_rows[0:1, 0:C], in_=norm2_g.rearrange("(o c) -> o c", o=1))
+        nc.scalar.dma_start(out=gb_rows[0:1, C : 2 * C], in_=norm2_b.rearrange("(o c) -> o c", o=1))
+        nc.scalar.dma_start(out=b_rows[0 : 2 * K, :].bitcast(BF16), in_=conv2_b.rearrange("(r x) -> r x", x=2 * P))
         nc.scalar.activation(out=warm2[:], in_=warm[:], func=ACT.Abs_reciprocal_sqrt)
 
-        def load_g(h, lo, hi):
-            if ROW2:
-                nc.sync.dma_start(
-                    out=g_sb[h][:, lo:hi, :].rearrange("p (d i) c -> p d (i c)", i=2),
-                    in_=g1[HALF * h + lo : HALF * h + hi].rearrange("b v c -> (b v) c").rearrange("(d p i) c -> p d (i c)", p=P, i=2),
-                )
-            else:
-                nc.sync.dma_start(out=g_sb[h][:, lo:hi, :], in_=g1[HALF * h + lo : HALF * h + hi].rearrange("b v c -> v b c"))
-
-        def load_w(q, lo, hi):
-            if ROW2:
-                nc.sync.dma_start(
-                    out=w_sb[q][:, lo:hi, :].rearrange("p (d i) c -> p d (i c)", i=2),
-                    in_=conv2_w[C * q + P * lo : C * q + P * hi, :].rearrange("(d p i) c -> p d (i c)", p=P, i=2),
-                )
-                return
+        def load_rows(tile, pair, rows):
             nc.sync.dma_start(
-                out=w_sb[q][:, lo:hi, :],
-                in_=conv2_w[C * q + P * lo : C * q + P * hi, :].rearrange("(j p) c -> p j c", p=P),
+                out=tile[:, 2 * pair : 2 * pair + 2, :].rearrange("p (d i) c -> p d (i c)", i=2),
+                in_=rows.rearrange("(d p i) c -> p d (i c)", p=P, i=2),
             )
 
-        def load_a(h):
+        def load_g(h):
+            for pair in range(2):
+                first = HALF * h + 2 * pair
+                load_rows(g_sb[h], pair, g1[first : first + 2].rearrange("b v c -> (b v) c"))
+
+        def load_w(q):
+            for pair in range(2):
+                first = C * q + 2 * P * pair
+                load_rows(w_sb[q], pair, conv2_w[first : first + 2 * P, :])
+
+        def load_adjacency(h):
             some = slice(HALF * h, HALF * (h + 1))
             nc.sync.dma_start(
                 out=a_raw[32:128, some].rearrange("p b t w -> p b (t w)"),
@@ -142,42 +100,22 @@ def tile_block_attention_guide_pb_kernel(tc, g1, res1, adj, spatial_adj, conv2_w
             )
             nc.sync.dma_start(out=a_raw[0:32, some], in_=adj[some].rearrange("b o (m t) w -> m (b o) t w", t=4))
 
-        for c in LOADS.split():
-            if c == "g0":
-                load_g(0, 0, 2)
-                load_g(0, 2, 4)
-            elif c[0] == "w":
-                for x in range(WS[int(c[1])]):
-                    load_w(int(c[1]), 4 * x // WS[int(c[1])], 4 * (x + 1) // WS[int(c[1])])
-            elif c == "g1":
-                for x in range(WS[4]):
-                    load_g(1, 4 * x // WS[4], 4 * (x + 1) // WS[4])
-            elif c[0] == "a":
-                if c == "a0":
-                    nc.sync.dma_start(out=gain[0:32, :], in_=s2.partition_broadcast(32))
-                load_a(int(c[1]))
-            elif c[0] == "r":
-                some = slice(HALF * int(c[1]), HALF * (int(c[1]) + 1))
-                nc.sync.dma_start(out=res_sb[:, some, :], in_=res1[some].rearrange("b w c -> w b c"))
-            elif c == "cr":
-                nc.sync.dma_start(out=c_rows[0:4, :], in_=norm2_g.rearrange("(j p) -> j p", p=P))
-                nc.sync.dma_start(out=c_rows[4:8, :], in_=norm2_b.rearrange("(j p) -> j p", p=P))
-            elif c == "gb":
-                nc.sync.dma_start(out=gam[:], in_=norm2_g.partition_broadcast(P))
-                nc.sync.dma_start(out=bet[:], in_=norm2_b.partition_broadcast(P))
+        load_g(0)
+        for q in range(K):
+            load_w(q)
+        load_g(1)
+        nc.sync.dma_start(out=gain[0:32, :], in_=s2.partition_broadcast(32))
+        for h in range(2):
+            load_adjacency(h)
+        for h in range(2):
+            some = slice(HALF * h, HALF * (h + 1))
+            nc.sync.dma_start(out=res_sb[:, some, :], in_=res1[some].rearrange("b w c -> w b c"))
 
         masks.make_identity(nc, ident_f[:])
-        if ROW2:
-            nc.vector.tensor_copy(
-                out=perm_f[:].rearrange("p (d u m) -> p d u m", d=2, u=2),
-                in_=ident_f[:].rearrange("p (d m u) -> p d u m", d=2, u=2),
-            )
-        else:
-            nc.vector.tensor_copy(
-                out=perm_f[:].rearrange("p (u m e) -> p u m e", u=2, e=2),
-                in_=ident_f[:].rearrange("p (m u e) -> p u m e", u=2, e=2),
-            )
-        nc.vector.tensor_copy(out=ident_b[:], in_=ident_f[:])
+        nc.vector.tensor_copy(
+            out=perm_f[:].rearrange("p (d u m) -> p d u m", d=2, u=2),
+            in_=ident_f[:].rearrange("p (d m u) -> p d u m", d=2, u=2),
+        )
 
         def bank_tile(shape, dtype):
             return psum.tile(shape, dtype, name="ps", tag="ps")
@@ -190,8 +128,16 @@ def tile_block_attention_guide_pb_kernel(tc, g1, res1, adj, spatial_adj, conv2_w
             nc.tensor.matmul(out=wide[:], lhsT=ones[:], rhs=gb_rows[:, C * i : C * (i + 1)], start=True, stop=True)
             live[("wide", i)] = wide
 
-        def keep_spread(i, vec):
-            nc.scalar.copy(out=vec[:], in_=live[("wide", i)][:])
+        def keep_spread(i):
+            nc.scalar.copy(out=(gam, bet)[i][:], in_=live[("wide", i)][:])
+
+        def turn_bias():
+            b_t = bank_tile([P, P], F32)
+            nc.tensor.transpose(b_t[:], b_rows[:], ident_f[:])
+            live["b_t"] = b_t
+
+        def keep_bias():
+            nc.vector.tensor_copy(out=bias_w[:], in_=live["b_t"][:, 0 : 2 * K])
 
         def copy_words(eng, dst, src):
             if eng == "V":
@@ -199,38 +145,27 @@ def tile_block_attention_guide_pb_kernel(tc, g1, res1, adj, spatial_adj, conv2_w
             else:
                 nc.scalar.copy(out=dst, in_=src)
 
-        def turn_rows(key, rows, ident, pair):
+        def turn_rows(key, rows, matrix, pair):
             tr = bank_tile([P, 2, 2, P], F32)
             for a in range(2):
                 words = rows[:, 2 * pair + a, :].bitcast(F32)
                 for u in range(2):
-                    nc.tensor.transpose(tr[:, a, u, :], words[:, u::2], ident[:])
+                    nc.tensor.transpose(tr[:, a, u, :], words[:, u::2], matrix[:])
             live[key] = tr
 
-        def empty_rows(key, grouped, pair, eng):
-            if ROW2 and key[0] != "w":
-                dst = grouped[:].bitcast(F32).rearrange("p (d r a u) -> p d r a u", d=2, a=2, u=2)
-                copy_words(eng, dst[:, pair], live[key][:].rearrange("p a u r -> p r a u"))
-                return
+        def empty_slots(key, grouped, pair, eng):
             dst = grouped[:].bitcast(F32).rearrange("p (a r u) -> p a r u", a=4, u=2)
             copy_words(eng, dst[:, 2 * pair : 2 * pair + 2], live[key][:].rearrange("p a u r -> p a r u"))
+
+        def empty_woven(key, grouped, pair, eng):
+            dst = grouped[:].bitcast(F32).rearrange("p (d r a u) -> p d r a u", d=2, a=2, u=2)
+            copy_words(eng, dst[:, pair], live[key][:].rearrange("p a u r -> p r a u"))
 
         def quantize(codes, scales, grouped):
             nc.vector.quantize_mx(out=codes[:].bitcast(FP8X4), scales=scales[:], in_=grouped[:])
 
-        def turn_bias():
-            b_t = bank_tile([P, P], F32 if ROW2 else BF16)
-            nc.tensor.transpose(b_t[:], b_rows[:], ident_f[:] if ROW2 else ident_b[:])
-            live["b_t"] = b_t
-
-        def keep_bias():
-            if ROW2:
-                nc.vector.tensor_copy(out=bias_w[:], in_=live["b_t"][:, 0:8])
-            else:
-                nc.vector.tensor_copy(out=bias_f[:], in_=live["b_t"][:, 0:16])
-
         def stage1(q, j, h):
-            bank = bank_tile([P, HALF * J], BANK_DT)
+            bank = bank_tile([P, HALF * J], BF16)
             cols = slice(P * j, P * (j + 1))
             nc.tensor.matmul_mx(
                 out=bank[:],
@@ -244,10 +179,9 @@ def tile_block_attention_guide_pb_kernel(tc, g1, res1, adj, spatial_adj, conv2_w
             live[("bank", q, j, h)] = bank
 
         def empty_bank(q, j, h):
-            bank = live[("bank", q, j, h)]
             dst = h_t[h][j][:].rearrange("p (b u k x) -> p b u k x", b=HALF, u=2, k=K)[:, :, :, q, :]
-            src = bank[:].rearrange("p (b u x) -> p b u x", b=HALF, u=2)
-            col = (bias_w[:].bitcast(BF16) if ROW2 else bias_f)[:, 4 * q + j : 4 * q + j + 1]
+            src = live[("bank", q, j, h)][:].rearrange("p (b u x) -> p b u x", b=HALF, u=2)
+            col = bias_w[:].bitcast(BF16)[:, CHUNKS * q + j : CHUNKS * q + j + 1]
             if j in ON_VECTOR[(h, q % 2)]:
                 nc.vector.tensor_scalar(out=dst, in0=src, scalar1=col, scalar2=None, op0=ALU.add)
             else:
@@ -264,9 +198,8 @@ def tile_block_attention_guide_pb_kernel(tc, g1, res1, adj, spatial_adj, conv2_w
 
         def empty_h(b, pair):
             if pair == 0:
-                h_in = work.tile([P, 4 * C], BF16, name="h_in", tag="h_in", align_bytes=64)
-                live[("h_in", b)] = h_in
-            empty_rows(("h", b, pair), live[("h_in", b)], pair, (RHR[b] if b < len(RHR) else RH)[pair])
+                live[("h_in", b)] = work.tile([P, 4 * C], BF16, name="h_in", tag="h_in", align_bytes=64)
+            empty_woven(("h", b, pair), live[("h_in", b)], pair, "S")
 
         def quantize_h(b):
             h_q = work.tile([P, C], U32, name="h_q", tag="h_q", align_bytes=64)
@@ -274,16 +207,14 @@ def tile_block_attention_guide_pb_kernel(tc, g1, res1, adj, spatial_adj, conv2_w
             quantize(h_q, h_s, live[("h_in", b)])
             live[("h_q", b)] = (h_q, h_s)
 
-        def weave(h, eng):
-            dst = a_in[h][:].rearrange("p (b w t) -> p b w t", b=HALF, t=4)
-            src = a_raw[:, HALF * h : HALF * (h + 1)].rearrange("p b t w -> p b w t")
-            if eng == "V":
-                nc.vector.tensor_scalar(out=dst, in0=src, scalar1=gain[:, 0:1], scalar2=None, op0=ALU.mult)
-            else:
-                nc.scalar.activation(out=dst, in_=src, func=ACT.Copy, scale=gain_f[:, 0:1])
-
-        def adjacency(h):
-            quantize(a_q[h], a_s[h], a_in[h])
+        def weave_adjacency(h):
+            nc.vector.tensor_scalar(
+                out=a_in[h][:].rearrange("p (b w t) -> p b w t", b=HALF, t=4),
+                in0=a_raw[:, HALF * h : HALF * (h + 1)].rearrange("p b t w -> p b w t"),
+                scalar1=gain[:, 0:1],
+                scalar2=None,
+                op0=ALU.mult,
+            )
 
         def stage2(b):
             h, bl = divmod(b, HALF)
@@ -302,31 +233,28 @@ def tile_block_attention_guide_pb_kernel(tc, g1, res1, adj, spatial_adj, conv2_w
             live[("acc", b)] = acc
 
         def residual(b):
-            x2 = lnp.tile([P, C], F32, name="x2", tag="x2")
-            total = lnp.tile([P, 1], F32, name="total", tag="total")
+            x2 = work.tile([P, C], F32, name="x2", tag="x2")
+            total = work.tile([P, 1], F32, name="total", tag="total")
             nc.vector.scalar_tensor_tensor(
                 out=x2[:], in0=live[("acc", b)][:], scalar=1.0, in1=res_sb[:, b, :],
                 op0=ALU.mult, op1=ALU.add, accum_out=total[:],
             )
             nc.sync.dma_start(out=out_0[b], in_=x2[:])
-            negm = lnp.tile([P, 1], F32, name="negm", tag="negm")
-            if GNEG:
-                nc.gpsimd.tensor_scalar(out=negm[:], in0=total[:], scalar1=-1.0 / C, scalar2=0.0, op0=ALU.mult, op1=ALU.add)
-            else:
-                nc.scalar.activation(out=negm[:], in_=total[:], func=ACT.Copy, scale=-1.0 / C)
+            negm = work.tile([P, 1], F32, name="negm", tag="negm")
+            nc.scalar.activation(out=negm[:], in_=total[:], func=ACT.Copy, scale=-1.0 / C)
             live[("x2", b)] = (x2, total, negm)
 
-        def spread_of(b):
+        def squares(b):
             x2, total, negm = live[("x2", b)]
-            junk = lnp.tile([P, C], BF16, name="junk", tag="junk")
-            ssq = lnp.tile([P, 1], F32, name="ssq", tag="ssq")
+            junk = work.tile([P, C], BF16, name="junk", tag="junk")
+            ssq = work.tile([P, 1], F32, name="ssq", tag="ssq")
             nc.scalar.activation(
                 out=junk[:], in_=x2[:], func=ACT.Square, bias=total[:, 0:1], scale=-1.0 * C, accum_out=ssq[:]
             )
             live[("ssq", b)] = ssq
 
-        def rstd_of(b):
-            rstd = lnp.tile([P, 1], F32, name="rstd", tag="rstd")
+        def inverse_deviation(b):
+            rstd = work.tile([P, 1], F32, name="rstd", tag="rstd")
             nc.scalar.activation(
                 out=rstd[:], in_=live[("ssq", b)][:], func=ACT.Abs_reciprocal_sqrt, bias=EPS, scale=1.0 / (C * C * C)
             )
@@ -334,169 +262,90 @@ def tile_block_attention_guide_pb_kernel(tc, g1, res1, adj, spatial_adj, conv2_w
 
         def centre(b):
             x2, total, negm = live[("x2", b)]
-            cen = lnp.tile([P, C], F32, name="cen", tag="cen")
+            cen = work.tile([P, C], F32, name="cen", tag="cen")
             nc.vector.scalar_tensor_tensor(
                 out=cen[:], in0=x2[:], scalar=negm[:, 0:1], in1=gam[:], op0=ALU.add, op1=ALU.mult
             )
             live[("cen", b)] = cen
 
         def finish(b):
-            xn = lnp.tile([P, C], F32, name="xn", tag="xn")
-            parts = TAIL if b == B - 1 else 1
-            for x in range(parts):
-                cols = slice(C * x // parts, C * (x + 1) // parts)
+            xn = work.tile([P, C], F32, name="xn", tag="xn")
+            pieces = LAST_PIECES if b == B - 1 else 1
+            for x in range(pieces):
+                cols = slice(C * x // pieces, C * (x + 1) // pieces)
                 nc.vector.scalar_tensor_tensor(
                     out=xn[:, cols], in0=live[("cen", b)][:, cols], scalar=live[("rstd", b)][:, 0:1], in1=bet[:, cols],
                     op0=ALU.mult, op1=ALU.add,
                 )
                 nc.sync.dma_start(out=out_1[b][:, cols], in_=xn[:, cols])
 
-        def turn_cols():
-            c_t = bank_tile([P, P], BF16)
-            nc.tensor.transpose(c_t[:], c_rows[:], ident_b[:])
-            nc.scalar.copy(out=cols_f[:], in_=c_t[:, 0:8])
-
-        def norm_rows(b):
-            x2, total, negm = live[("x2", b)]
-            rstd = live[("rstd", b)]
-            nmr = work.tile([P, 1], F32, name="nmr", tag="nmr")
-            nc.scalar.activation(out=nmr[:], in_=negm[:], func=ACT.Copy, scale=rstd[:, 0:1])
-            xh = work.tile([P, C], F32, name="xh", tag="xh")
-            nc.scalar.activation(out=xh[:], in_=x2[:], func=ACT.Identity, bias=nmr[:, 0:1], scale=rstd[:, 0:1])
-            tx = bank_tile([P, 4, P], F32)
-            for j in range(4):
-                nc.tensor.transpose(tx[:, j, :], xh[:, P * j : P * (j + 1)], ident_f[:])
-            live[("tx", b)] = tx
-
-        def gain_cols(b):
-            y_t = work.tile([P, 4, P], F32, name="y_t", tag="y_t")
-            for j in range(4):
-                nc.scalar.activation(
-                    out=y_t[:, j, :], in_=live[("tx", b)][:, j, :], func=ACT.Identity,
-                    bias=cols_f[:, 4 + j : 5 + j], scale=cols_f[:, j : j + 1],
-                )
-            ty = bank_tile([P, 4, P], F32)
-            for j in range(4):
-                nc.tensor.transpose(ty[:, j, :], y_t[:, j, :], ident_f[:])
-            live[("ty", b)] = ty
-
-        def keep_norm(b):
-            xn = lnp.tile([P, C], F32, name="xn", tag="xn")
-            nc.scalar.copy(out=xn[:], in_=live[("ty", b)][:].rearrange("p j c -> p (j c)"))
-            nc.sync.dma_start(out=out_1[b], in_=xn[:])
-
         for i in range(WARM_UP):
             spin()
-        if EGB:
-            spread(0)
-            spread(1)
-            turn_bias()
-            keep_spread(0, gam)
-            keep_spread(1, bet)
-            keep_bias()
 
-        seq = [("g", 0), ("w", 0), ("w", 1), ("w", 2), ("w", 3), ("g", 1)]
-        src = {"g": g_sb, "w": w_sb}
-        mat = {"g": perm_f, "w": ident_f}
-        dst = {"g": (g_in, g_q, g_s), "w": (w_in, w_q, w_s)}
-        for i in range(len(seq) + AH):
-            if i < len(seq):
-                kind, n = seq[i]
+        sources = [(g_sb[0], perm_f, empty_woven, g_in[0], g_q[0], g_s[0])]
+        sources += [(w_sb[q], ident_f, empty_slots, w_in[q], w_q[q], w_s[q]) for q in range(K)]
+        sources += [(g_sb[1], perm_f, empty_woven, g_in[1], g_q[1], g_s[1])]
+        for i in range(len(sources) + LEAD):
+            q = i - 1 - LEAD
+            if i < len(sources):
+                rows, matrix, empty, grouped, codes, scales = sources[i]
                 for pair in range(2):
-                    turn_rows((kind, n, pair), src[kind][n], mat[kind], pair)
-                    if GB == "pe" and i == 1 and pair == 0 and not EGB:
+                    turn_rows(("t", i, pair), rows, matrix, pair)
+                    if i == 1 and pair == 0:
                         spread(1)
-                    if i < len(SPINS) and SPINS[i] == 2:
-                        spin()
-                if i == 0 and not EGB:
-                    if GB == "pe":
-                        spread(0)
+                if i == 0:
+                    spread(0)
                     turn_bias()
-                for x in range(SPINS[i] if i < len(SPINS) and SPINS[i] != 2 else 0):
-                    spin()
-            q = i - 1 - AH
             if 0 <= q < K:
-                for j in range(4):
+                for j in range(CHUNKS):
                     stage1(q, j, 0)
-            vfirst = [j for j in range(4) if 0 <= q < K and j in ON_VECTOR[(0, q % 2)]][:NB]
-            if i < len(seq):
-                grouped, codes, scales = dst[kind]
-                empty_rows((kind, n, 0), grouped[n], 0, RD0[i])
-                if i == 0 and not EGB:
+            first = 0
+            if i < len(sources):
+                empty(("t", i, 0), grouped, 0, "V")
+                if i == 0:
                     keep_bias()
-                empty_rows((kind, n, 1), grouped[n], 1, RD[i])
-                if GB == "pe" and i < 2 and not EGB:
-                    keep_spread(i, (gam, bet)[i])
-                if i == 1 and LAG:
+                empty(("t", i, 1), grouped, 1, "S")
+                if i < 2:
+                    keep_spread(i)
+                if i == 1:
                     quantize(g_q[0], g_s[0], g_in[0])
-                for j in vfirst:
-                    empty_bank(q, j, 0)
-                if not (i == 0 and LAG):
-                    quantize(codes[n], scales[n], grouped[n])
+                if 0 <= q < K:
+                    empty_bank(q, 0, 0)
+                    first = 1
+                if i > 0:
+                    quantize(codes, scales, grouped)
             if 0 <= q < K:
-                for j in range(4):
-                    if i >= len(seq) or j not in vfirst:
-                        empty_bank(q, j, 0)
-            for h in range(2):
-                if WVP[h] == i - len(seq) - AH:
-                    if WVE[h] == "S":
-                        nc.vector.tensor_copy(out=gain_f[:], in_=gain[:])
-                    weave(h, WVE[h])
-            for h in range(2):
-                if AQ[h] == i - len(seq) - AH:
-                    adjacency(h)
+                for j in range(first, CHUNKS):
+                    empty_bank(q, j, 0)
+            if i >= len(sources):
+                weave_adjacency(i - len(sources))
 
-        for i in range(B + max(max(OFF), SOFF[2] if SL else 0)):
-            late = LATE[i] if i < len(LATE) else ()
-            if SL and i == 3:
-                turn_cols()
-            if SQ1 and 0 <= i - OFF[2] < B:
-                spread_of(i - OFF[2])
+        for i in range(B + FINISH_LAG):
+            late = LATE_SLICES[i] if i < len(LATE_SLICES) else ()
             if i < B:
                 for pair in range(2):
                     turn_h(i, pair)
                 for pair in range(2):
                     empty_h(i, pair)
-            if SQ1 and 0 <= i - OFF[2] < B:
-                rstd_of(i - OFF[2])
             for q in late:
-                for j in range(4):
+                for j in range(CHUNKS):
                     stage1(q, j, 1)
             for h in range(2):
-                if WVP[h] == i:
-                    if WVE[h] == "S":
-                        nc.vector.tensor_copy(out=gain_f[:], in_=gain[:])
-                    weave(h, WVE[h])
-            for h in range(2):
-                if AQ[h] == i:
-                    adjacency(h)
-            if 0 <= i - OFF[0] < B:
-                quantize_h(i - OFF[0])
-                stage2(i - OFF[0])
-            if not SLAST and i - SOFF[2] in SL:
-                keep_norm(i - SOFF[2])
-            if not SLAST and i - SOFF[1] in SL:
-                gain_cols(i - SOFF[1])
-            if not SQ1 and 0 <= i - OFF[2] < B:
-                spread_of(i - OFF[2])
-                if not SQ2:
-                    rstd_of(i - OFF[2])
-            if not SLAST and i - SOFF[0] in SL:
-                norm_rows(i - SOFF[0])
+                if ADJ_ROUND[h] == i:
+                    quantize(a_q[h], a_s[h], a_in[h])
+            if 0 <= i - QUANTISE_LAG < B:
+                quantize_h(i - QUANTISE_LAG)
+                stage2(i - QUANTISE_LAG)
+            if 0 <= i - STATS_LAG < B:
+                squares(i - STATS_LAG)
             for q in late:
-                for j in range(4):
+                for j in range(CHUNKS):
                     empty_bank(q, j, 1)
-            if 0 <= i - OFF[1] < B:
-                residual(i - OFF[1])
-            if SQ2 and 0 <= i - OFF[2] < B:
-                rstd_of(i - OFF[2])
-            if 0 <= i - OFF[3] < B and i - OFF[3] not in SL:
-                centre(i - OFF[3])
-            if 0 <= i - OFF[4] < B and i - OFF[4] not in SL:
-                finish(i - OFF[4])
-            if SLAST and i - SOFF[2] in SL:
-                keep_norm(i - SOFF[2])
-            if SLAST and i - SOFF[1] in SL:
-                gain_cols(i - SOFF[1])
-            if SLAST and i - SOFF[0] in SL:
-                norm_rows(i - SOFF[0])
+            if 0 <= i - RESIDUAL_LAG < B:
+                residual(i - RESIDUAL_LAG)
+            if 0 <= i - STATS_LAG < B:
+                inverse_deviation(i - STATS_LAG)
+            if 0 <= i - CENTRE_LAG < B:
+                centre(i - CENTRE_LAG)
+            if 0 <= i - FINISH_LAG < B:
+                finish(i - FINISH_LAG)

@@ -15,6 +15,7 @@ B, J, C, K = 8, 128, 512, 4
 EPS = 1e-5
 P = 128
 HALF = 4
+QUAD = J // 4
 CHUNKS = 4
 
 FLOPS = 2 * B * J * C * K * C + 2 * B * J * K * J * C
@@ -37,8 +38,8 @@ def tile_block_attention_guide_pb_kernel(tc, g1, res1, adj, spatial_adj, conv2_w
         psum = ctx.enter_context(tc.psum_pool(name="psum", bufs=8))
         ctx.enter_context(tc.manual_schedule())
 
-        g_sb = [keep.tile([P, HALF, C], BF16, name="g_sb%d" % h) for h in range(2)]
-        w_sb = [keep.tile([P, CHUNKS, C], BF16, name="w_sb%d" % q) for q in range(K)]
+        g_sb = [keep.tile([P, HALF, C], BF16, name="g_sb%d" % half) for half in range(2)]
+        w_sb = [keep.tile([P, CHUNKS, C], BF16, name="w_sb%d" % k) for k in range(K)]
         a_raw = keep.tile([P, B, 4, J], BF16, name="a_raw")
         res_sb = keep.tile([P, B, C], BF16, name="res_sb")
         b_rows = keep.tile([P, P], F32, name="b_rows")
@@ -53,16 +54,16 @@ def tile_block_attention_guide_pb_kernel(tc, g1, res1, adj, spatial_adj, conv2_w
         bet = keep.tile([P, C], BF16, name="bet")
         ident_f = keep.tile([P, P], F32, name="ident_f")
         perm_f = keep.tile([P, P], F32, name="perm_f")
-        g_in = [keep.tile([P, 4 * C], BF16, name="g_in%d" % h, align_bytes=64) for h in range(2)]
-        g_q = [keep.tile([P, C], U32, name="g_q%d" % h, align_bytes=64) for h in range(2)]
-        g_s = [keep.tile([P, C], U8, name="g_s%d" % h, align_bytes=64) for h in range(2)]
-        w_in = [keep.tile([P, 4 * C], BF16, name="w_in%d" % q, align_bytes=64) for q in range(K)]
-        w_q = [keep.tile([P, C], U32, name="w_q%d" % q, align_bytes=64) for q in range(K)]
-        w_s = [keep.tile([P, C], U8, name="w_s%d" % q, align_bytes=64) for q in range(K)]
-        a_in = [keep.tile([P, HALF * J * 4], BF16, name="a_in%d" % h, align_bytes=64) for h in range(2)]
-        a_q = [keep.tile([P, HALF * J], U32, name="a_q%d" % h, align_bytes=64) for h in range(2)]
-        a_s = [keep.tile([P, HALF * J], U8, name="a_s%d" % h, align_bytes=64) for h in range(2)]
-        h_t = [[keep.tile([P, HALF * C], BF16, name="h_t%d_%d" % (h, j)) for j in range(CHUNKS)] for h in range(2)]
+        g_in = [keep.tile([P, 4 * C], BF16, name="g_in%d" % half, align_bytes=64) for half in range(2)]
+        g_q = [keep.tile([P, C], U32, name="g_q%d" % half, align_bytes=64) for half in range(2)]
+        g_s = [keep.tile([P, C], U8, name="g_s%d" % half, align_bytes=64) for half in range(2)]
+        w_in = [keep.tile([P, 4 * C], BF16, name="w_in%d" % k, align_bytes=64) for k in range(K)]
+        w_q = [keep.tile([P, C], U32, name="w_q%d" % k, align_bytes=64) for k in range(K)]
+        w_s = [keep.tile([P, C], U8, name="w_s%d" % k, align_bytes=64) for k in range(K)]
+        a_in = [keep.tile([P, HALF * J * 4], BF16, name="a_in%d" % half, align_bytes=64) for half in range(2)]
+        a_q = [keep.tile([P, HALF * J], U32, name="a_q%d" % half, align_bytes=64) for half in range(2)]
+        a_s = [keep.tile([P, HALF * J], U8, name="a_s%d" % half, align_bytes=64) for half in range(2)]
+        h_t = [[keep.tile([P, HALF * C], BF16, name="h_t%d_%d" % (half, j)) for j in range(CHUNKS)] for half in range(2)]
         live = {}
 
         nc.vector.memset(ones[:], 1.0)
@@ -76,45 +77,45 @@ def tile_block_attention_guide_pb_kernel(tc, g1, res1, adj, spatial_adj, conv2_w
         nc.scalar.dma_start(out=b_rows[0 : 2 * K, :].bitcast(BF16), in_=conv2_b.rearrange("(r x) -> r x", x=2 * P))
         nc.scalar.activation(out=warm2[:], in_=warm[:], func=ACT.Abs_reciprocal_sqrt)
 
-        def load_rows(tile, pair, rows):
+        def load_rows(loaded, pair, hbm_rows):
             nc.sync.dma_start(
-                out=tile[:, 2 * pair : 2 * pair + 2, :].rearrange("p (d i) c -> p d (i c)", i=2),
-                in_=rows.rearrange("(d p i) c -> p d (i c)", p=P, i=2),
+                out=loaded[:, 2 * pair : 2 * pair + 2, :].rearrange("p (o a) c -> p o (a c)", a=2),
+                in_=hbm_rows.rearrange("(o p a) c -> p o (a c)", p=P, a=2),
             )
 
-        def load_g(h):
+        def load_g(half):
             for pair in range(2):
-                first = HALF * h + 2 * pair
-                load_rows(g_sb[h], pair, g1[first : first + 2].rearrange("b v c -> (b v) c"))
+                sample = HALF * half + 2 * pair
+                load_rows(g_sb[half], pair, g1[sample : sample + 2].rearrange("b v c -> (b v) c"))
 
-        def load_w(q):
+        def load_w(k):
             for pair in range(2):
-                first = C * q + 2 * P * pair
-                load_rows(w_sb[q], pair, conv2_w[first : first + 2 * P, :])
+                row = C * k + 2 * P * pair
+                load_rows(w_sb[k], pair, conv2_w[row : row + 2 * P, :])
 
-        def load_adjacency(h):
-            some = slice(HALF * h, HALF * (h + 1))
+        def load_adjacency(half):
+            some = slice(HALF * half, HALF * (half + 1))
             nc.sync.dma_start(
-                out=a_raw[32:128, some].rearrange("p b t w -> p b (t w)"),
-                in_=spatial_adj.rearrange("k (m t) w -> (k m) (t w)", t=4).unsqueeze(1).to_broadcast([96, HALF, 4 * J]),
+                out=a_raw[QUAD:P, some].rearrange("p b t w -> p b (t w)"),
+                in_=spatial_adj.rearrange("k (m t) w -> (k m) (t w)", t=4).unsqueeze(1).to_broadcast([P - QUAD, HALF, 4 * J]),
             )
-            nc.sync.dma_start(out=a_raw[0:32, some], in_=adj[some].rearrange("b o (m t) w -> m (b o) t w", t=4))
+            nc.sync.dma_start(out=a_raw[0:QUAD, some], in_=adj[some].rearrange("b o (m t) w -> m (b o) t w", t=4))
 
         load_g(0)
-        for q in range(K):
-            load_w(q)
+        for k in range(K):
+            load_w(k)
         load_g(1)
-        nc.sync.dma_start(out=gain[0:32, :], in_=s2.partition_broadcast(32))
-        for h in range(2):
-            load_adjacency(h)
-        for h in range(2):
-            some = slice(HALF * h, HALF * (h + 1))
+        nc.sync.dma_start(out=gain[0:QUAD, :], in_=s2.partition_broadcast(QUAD))
+        for half in range(2):
+            load_adjacency(half)
+        for half in range(2):
+            some = slice(HALF * half, HALF * (half + 1))
             nc.sync.dma_start(out=res_sb[:, some, :], in_=res1[some].rearrange("b w c -> w b c"))
 
         masks.make_identity(nc, ident_f[:])
         nc.vector.tensor_copy(
-            out=perm_f[:].rearrange("p (d u m) -> p d u m", d=2, u=2),
-            in_=ident_f[:].rearrange("p (d m u) -> p d u m", d=2, u=2),
+            out=perm_f[:].rearrange("p (n u m) -> p n u m", n=2, u=2),
+            in_=ident_f[:].rearrange("p (n m u) -> p n u m", n=2, u=2),
         )
 
         def bank_tile(shape, dtype):
@@ -123,13 +124,13 @@ def tile_block_attention_guide_pb_kernel(tc, g1, res1, adj, spatial_adj, conv2_w
         def spin():
             nc.tensor.matmul(out=bank_tile([P, C], F32)[:], lhsT=ones[:], rhs=idle[:], start=True, stop=True)
 
-        def spread(i):
+        def spread(which):
             wide = bank_tile([P, C], F32)
-            nc.tensor.matmul(out=wide[:], lhsT=ones[:], rhs=gb_rows[:, C * i : C * (i + 1)], start=True, stop=True)
-            live[("wide", i)] = wide
+            nc.tensor.matmul(out=wide[:], lhsT=ones[:], rhs=gb_rows[:, C * which : C * (which + 1)], start=True, stop=True)
+            live[("wide", which)] = wide
 
-        def keep_spread(i):
-            nc.scalar.copy(out=(gam, bet)[i][:], in_=live[("wide", i)][:])
+        def keep_spread(which):
+            nc.scalar.copy(out=(gam, bet)[which][:], in_=live[("wide", which)][:])
 
         def turn_bias():
             b_t = bank_tile([P, P], F32)
@@ -145,10 +146,10 @@ def tile_block_attention_guide_pb_kernel(tc, g1, res1, adj, spatial_adj, conv2_w
             else:
                 nc.scalar.copy(out=dst, in_=src)
 
-        def turn_rows(key, rows, matrix, pair):
+        def turn_rows(key, loaded, matrix, pair):
             tr = bank_tile([P, 2, 2, P], F32)
             for a in range(2):
-                words = rows[:, 2 * pair + a, :].bitcast(F32)
+                words = loaded[:, 2 * pair + a, :].bitcast(F32)
                 for u in range(2):
                     nc.tensor.transpose(tr[:, a, u, :], words[:, u::2], matrix[:])
             live[key] = tr
@@ -158,42 +159,42 @@ def tile_block_attention_guide_pb_kernel(tc, g1, res1, adj, spatial_adj, conv2_w
             copy_words(eng, dst[:, 2 * pair : 2 * pair + 2], live[key][:].rearrange("p a u r -> p a r u"))
 
         def empty_woven(key, grouped, pair, eng):
-            dst = grouped[:].bitcast(F32).rearrange("p (d r a u) -> p d r a u", d=2, a=2, u=2)
+            dst = grouped[:].bitcast(F32).rearrange("p (o r a u) -> p o r a u", o=2, a=2, u=2)
             copy_words(eng, dst[:, pair], live[key][:].rearrange("p a u r -> p r a u"))
 
         def quantize(codes, scales, grouped):
             nc.vector.quantize_mx(out=codes[:].bitcast(FP8X4), scales=scales[:], in_=grouped[:])
 
-        def stage1(q, j, h):
+        def stage1(k, j, half):
             bank = bank_tile([P, HALF * J], BF16)
             cols = slice(P * j, P * (j + 1))
             nc.tensor.matmul_mx(
                 out=bank[:],
-                lhsT=w_q[q][:, cols].bitcast(FP8X4),
-                lhsT_scale=w_s[q][:, cols],
-                rhs=g_q[h][:].bitcast(FP8X4),
-                rhs_scale=g_s[h][:],
+                lhsT=w_q[k][:, cols].bitcast(FP8X4),
+                lhsT_scale=w_s[k][:, cols],
+                rhs=g_q[half][:].bitcast(FP8X4),
+                rhs_scale=g_s[half][:],
                 start=True,
                 stop=True,
             )
-            live[("bank", q, j, h)] = bank
+            live[("bank", k, j, half)] = bank
 
-        def empty_bank(q, j, h):
-            dst = h_t[h][j][:].rearrange("p (b u k x) -> p b u k x", b=HALF, u=2, k=K)[:, :, :, q, :]
-            src = live[("bank", q, j, h)][:].rearrange("p (b u x) -> p b u x", b=HALF, u=2)
-            col = bias_w[:].bitcast(BF16)[:, CHUNKS * q + j : CHUNKS * q + j + 1]
-            if j in ON_VECTOR[(h, q % 2)]:
+        def empty_bank(k, j, half):
+            dst = h_t[half][j][:].rearrange("p (b u k x) -> p b u k x", b=HALF, u=2, k=K)[:, :, :, k, :]
+            src = live[("bank", k, j, half)][:].rearrange("p (b u x) -> p b u x", b=HALF, u=2)
+            col = bias_w[:].bitcast(BF16)[:, CHUNKS * k + j : CHUNKS * k + j + 1]
+            if j in ON_VECTOR[(half, k % 2)]:
                 nc.vector.tensor_scalar(out=dst, in0=src, scalar1=col, scalar2=None, op0=ALU.add)
             else:
                 nc.scalar.activation(out=dst, in_=src, func=ACT.Identity, bias=col, scale=1.0)
 
         def turn_h(b, pair):
-            h, bl = divmod(b, HALF)
+            half, bl = divmod(b, HALF)
             tr = bank_tile([P, 2, 2, P], F32)
             for a in range(2):
-                rows = h_t[h][2 * pair + a][:].rearrange("p (b u x) -> p b u x", b=HALF, u=2)
+                chunk = h_t[half][2 * pair + a][:].rearrange("p (b u x) -> p b u x", b=HALF, u=2)
                 for u in range(2):
-                    nc.tensor.transpose(tr[:, a, u, :], rows[:, bl, u, :].bitcast(F32), ident_f[:])
+                    nc.tensor.transpose(tr[:, a, u, :], chunk[:, bl, u, :].bitcast(F32), ident_f[:])
             live[("h", b, pair)] = tr
 
         def empty_h(b, pair):
@@ -207,24 +208,25 @@ def tile_block_attention_guide_pb_kernel(tc, g1, res1, adj, spatial_adj, conv2_w
             quantize(h_q, h_s, live[("h_in", b)])
             live[("h_q", b)] = (h_q, h_s)
 
-        def weave_adjacency(h):
+        def weave_adjacency(b):
+            half, bl = divmod(b, HALF)
             nc.vector.tensor_scalar(
-                out=a_in[h][:].rearrange("p (b w t) -> p b w t", b=HALF, t=4),
-                in0=a_raw[:, HALF * h : HALF * (h + 1)].rearrange("p b t w -> p b w t"),
+                out=a_in[half][:].rearrange("p (b c i t) -> p b c t i", b=HALF, i=4, t=4)[:, bl],
+                in0=a_raw[:, b].rearrange("p t (c i) -> p c t i", i=4),
                 scalar1=gain[:, 0:1],
                 scalar2=None,
                 op0=ALU.mult,
             )
 
         def stage2(b):
-            h, bl = divmod(b, HALF)
+            half, bl = divmod(b, HALF)
             h_q, h_s = live[("h_q", b)]
             acc = bank_tile([P, C], F32)
             cols = slice(J * bl, J * (bl + 1))
             nc.tensor.matmul_mx(
                 out=acc[:],
-                lhsT=a_q[h][:, cols].bitcast(FP8X4),
-                lhsT_scale=a_s[h][:, cols],
+                lhsT=a_q[half][:, cols].bitcast(FP8X4),
+                lhsT_scale=a_s[half][:, cols],
                 rhs=h_q[:].bitcast(FP8X4),
                 rhs_scale=h_s[:],
                 start=True,
@@ -271,81 +273,82 @@ def tile_block_attention_guide_pb_kernel(tc, g1, res1, adj, spatial_adj, conv2_w
         def finish(b):
             xn = work.tile([P, C], F32, name="xn", tag="xn")
             pieces = LAST_PIECES if b == B - 1 else 1
-            for x in range(pieces):
-                cols = slice(C * x // pieces, C * (x + 1) // pieces)
+            for piece in range(pieces):
+                cols = slice(C * piece // pieces, C * (piece + 1) // pieces)
                 nc.vector.scalar_tensor_tensor(
                     out=xn[:, cols], in0=live[("cen", b)][:, cols], scalar=live[("rstd", b)][:, 0:1], in1=bet[:, cols],
                     op0=ALU.mult, op1=ALU.add,
                 )
                 nc.sync.dma_start(out=out_1[b][:, cols], in_=xn[:, cols])
 
-        for i in range(WARM_UP):
+        for step in range(WARM_UP):
             spin()
 
         sources = [(g_sb[0], perm_f, empty_woven, g_in[0], g_q[0], g_s[0])]
-        sources += [(w_sb[q], ident_f, empty_slots, w_in[q], w_q[q], w_s[q]) for q in range(K)]
+        sources += [(w_sb[k], ident_f, empty_slots, w_in[k], w_q[k], w_s[k]) for k in range(K)]
         sources += [(g_sb[1], perm_f, empty_woven, g_in[1], g_q[1], g_s[1])]
-        for i in range(len(sources) + LEAD):
-            q = i - 1 - LEAD
-            if i < len(sources):
-                rows, matrix, empty, grouped, codes, scales = sources[i]
+        for step in range(len(sources) + LEAD):
+            k = step - 1 - LEAD
+            if step < len(sources):
+                loaded, matrix, empty, grouped, codes, scales = sources[step]
                 for pair in range(2):
-                    turn_rows(("t", i, pair), rows, matrix, pair)
-                    if i == 1 and pair == 0:
+                    turn_rows(("turned", step, pair), loaded, matrix, pair)
+                    if step == 1 and pair == 0:
                         spread(1)
-                if i == 0:
+                if step == 0:
                     spread(0)
                     turn_bias()
-            if 0 <= q < K:
+            if 0 <= k < K:
                 for j in range(CHUNKS):
-                    stage1(q, j, 0)
-            first = 0
-            if i < len(sources):
-                empty(("t", i, 0), grouped, 0, "V")
-                if i == 0:
+                    stage1(k, j, 0)
+            emptied = 0
+            if step < len(sources):
+                empty(("turned", step, 0), grouped, 0, "V")
+                if step == 0:
                     keep_bias()
-                empty(("t", i, 1), grouped, 1, "S")
-                if i < 2:
-                    keep_spread(i)
-                if i == 1:
+                empty(("turned", step, 1), grouped, 1, "S")
+                if step < 2:
+                    keep_spread(step)
+                if step == 1:
                     quantize(g_q[0], g_s[0], g_in[0])
-                if 0 <= q < K:
-                    empty_bank(q, 0, 0)
-                    first = 1
-                if i > 0:
+                if 0 <= k < K:
+                    empty_bank(k, 0, 0)
+                    emptied = 1
+                if step > 0:
                     quantize(codes, scales, grouped)
-            if 0 <= q < K:
-                for j in range(first, CHUNKS):
-                    empty_bank(q, j, 0)
-            if i >= len(sources):
-                weave_adjacency(i - len(sources))
+            if 0 <= k < K:
+                for j in range(emptied, CHUNKS):
+                    empty_bank(k, j, 0)
+            if step >= len(sources):
+                for bl in range(HALF):
+                    weave_adjacency(HALF * (step - len(sources)) + bl)
 
-        for i in range(B + FINISH_LAG):
-            late = LATE_SLICES[i] if i < len(LATE_SLICES) else ()
-            if i < B:
+        for rnd in range(B + FINISH_LAG):
+            late = LATE_SLICES[rnd] if rnd < len(LATE_SLICES) else ()
+            if rnd < B:
                 for pair in range(2):
-                    turn_h(i, pair)
+                    turn_h(rnd, pair)
                 for pair in range(2):
-                    empty_h(i, pair)
-            for q in late:
+                    empty_h(rnd, pair)
+            for k in late:
                 for j in range(CHUNKS):
-                    stage1(q, j, 1)
-            for h in range(2):
-                if ADJ_ROUND[h] == i:
-                    quantize(a_q[h], a_s[h], a_in[h])
-            if 0 <= i - QUANTISE_LAG < B:
-                quantize_h(i - QUANTISE_LAG)
-                stage2(i - QUANTISE_LAG)
-            if 0 <= i - STATS_LAG < B:
-                squares(i - STATS_LAG)
-            for q in late:
+                    stage1(k, j, 1)
+            for half in range(2):
+                if ADJ_ROUND[half] == rnd:
+                    quantize(a_q[half], a_s[half], a_in[half])
+            if 0 <= rnd - QUANTISE_LAG < B:
+                quantize_h(rnd - QUANTISE_LAG)
+                stage2(rnd - QUANTISE_LAG)
+            if 0 <= rnd - STATS_LAG < B:
+                squares(rnd - STATS_LAG)
+            for k in late:
                 for j in range(CHUNKS):
-                    empty_bank(q, j, 1)
-            if 0 <= i - RESIDUAL_LAG < B:
-                residual(i - RESIDUAL_LAG)
-            if 0 <= i - STATS_LAG < B:
-                inverse_deviation(i - STATS_LAG)
-            if 0 <= i - CENTRE_LAG < B:
-                centre(i - CENTRE_LAG)
-            if 0 <= i - FINISH_LAG < B:
-                finish(i - FINISH_LAG)
+                    empty_bank(k, j, 1)
+            if 0 <= rnd - RESIDUAL_LAG < B:
+                residual(rnd - RESIDUAL_LAG)
+            if 0 <= rnd - STATS_LAG < B:
+                inverse_deviation(rnd - STATS_LAG)
+            if 0 <= rnd - CENTRE_LAG < B:
+                centre(rnd - CENTRE_LAG)
+            if 0 <= rnd - FINISH_LAG < B:
+                finish(rnd - FINISH_LAG)

@@ -21,7 +21,7 @@ CHUNKS = 4
 FLOPS = 2 * B * J * C * K * C + 2 * B * J * K * J * C
 
 ON_VECTOR = {(0, 0): (0, 3), (0, 1): (0, 3), (1, 0): (1, 2, 3), (1, 1): (0, 1)}
-WARM_UP = 6
+WARM_UP = 3
 LEAD = 2
 LATE_SLICES = ((0, 1), (2,), (3,))
 ADJ_ROUND = (0, 2)
@@ -66,15 +66,14 @@ def tile_block_attention_guide_pb_kernel(tc, g1, res1, adj, spatial_adj, conv2_w
         h_t = [[keep.tile([P, HALF * C], BF16, name="h_t%d_%d" % (half, j)) for j in range(CHUNKS)] for half in range(2)]
         live = {}
 
-        nc.vector.memset(ones[:], 1.0)
-        nc.vector.memset(idle[:], 0.0)
-        nc.vector.memset(gb_rows[:], 0.0)
+        nc.vector.memset(idle[:].bitcast(F32), 0.0)
         nc.vector.memset(b_rows[:], 0.0)
-        nc.vector.memset(gain[:], 1.0)
+        nc.vector.memset(gb_rows[:].bitcast(F32), 0.0)
         nc.vector.memset(warm[:], 1.0)
+        nc.vector.memset(gain[:], 1.0)
+        nc.scalar.dma_start(out=b_rows[0 : 2 * K, :].bitcast(BF16), in_=conv2_b.rearrange("(r x) -> r x", x=2 * P))
         nc.scalar.dma_start(out=gb_rows[0:1, 0:C], in_=norm2_g.rearrange("(o c) -> o c", o=1))
         nc.scalar.dma_start(out=gb_rows[0:1, C : 2 * C], in_=norm2_b.rearrange("(o c) -> o c", o=1))
-        nc.scalar.dma_start(out=b_rows[0 : 2 * K, :].bitcast(BF16), in_=conv2_b.rearrange("(r x) -> r x", x=2 * P))
         nc.scalar.activation(out=warm2[:], in_=warm[:], func=ACT.Abs_reciprocal_sqrt)
 
         def load_rows(loaded, pair, hbm_rows):
@@ -118,11 +117,13 @@ def tile_block_attention_guide_pb_kernel(tc, g1, res1, adj, spatial_adj, conv2_w
             in_=ident_f[:].rearrange("p (n m u) -> p n u m", n=2, u=2),
         )
 
+        nc.vector.memset(ones[:], 1.0)
+
         def bank_tile(shape, dtype):
             return psum.tile(shape, dtype, name="ps", tag="ps")
 
         def spin():
-            nc.tensor.matmul(out=bank_tile([P, C], F32)[:], lhsT=ones[:], rhs=idle[:], start=True, stop=True)
+            nc.tensor.matmul(out=bank_tile([P, C], F32)[:], lhsT=idle[:, 0:P], rhs=idle[:], start=True, stop=True)
 
         def spread(which):
             wide = bank_tile([P, C], F32)
@@ -293,22 +294,22 @@ def tile_block_attention_guide_pb_kernel(tc, g1, res1, adj, spatial_adj, conv2_w
                 loaded, matrix, empty, grouped, codes, scales = sources[step]
                 for pair in range(2):
                     turn_rows(("turned", step, pair), loaded, matrix, pair)
-                    if step == 1 and pair == 0:
-                        spread(1)
-                if step == 0:
-                    spread(0)
+                if step == 1:
                     turn_bias()
+                    spread(0)
+                if step == 2:
+                    spread(1)
             if 0 <= k < K:
                 for j in range(CHUNKS):
                     stage1(k, j, 0)
             emptied = 0
             if step < len(sources):
                 empty(("turned", step, 0), grouped, 0, "V")
-                if step == 0:
+                if step == 1:
                     keep_bias()
                 empty(("turned", step, 1), grouped, 1, "S")
-                if step < 2:
-                    keep_spread(step)
+                if step in (1, 2):
+                    keep_spread(step - 1)
                 if step == 1:
                     quantize(g_q[0], g_s[0], g_in[0])
                 if 0 <= k < K:

@@ -21,7 +21,7 @@ CHUNKS = 4
 FLOPS = 2 * B * J * C * K * C + 2 * B * J * K * J * C
 
 ON_VECTOR = {(0, 0): (0, 3), (0, 1): (0, 3), (1, 0): (1, 2, 3), (1, 1): (0, 1)}
-WARM_UP = 3
+WARM_UP = 4
 LEAD = 2
 LATE_SLICES = ((0, 1), (2,), (3,))
 ADJ_ROUND = (0, 2)
@@ -296,8 +296,8 @@ def tile_block_attention_guide_pb_kernel(tc, g1, res1, adj, spatial_adj, conv2_w
                     turn_rows(("turned", step, pair), loaded, matrix, pair)
                 if step == 1:
                     turn_bias()
-                    spread(0)
                 if step == 2:
+                    spread(0)
                     spread(1)
             if 0 <= k < K:
                 for j in range(CHUNKS):
@@ -308,8 +308,8 @@ def tile_block_attention_guide_pb_kernel(tc, g1, res1, adj, spatial_adj, conv2_w
                 if step == 1:
                     keep_bias()
                 empty(("turned", step, 1), grouped, 1, "S")
-                if step in (1, 2):
-                    keep_spread(step - 1)
+                if step in (2, 3):
+                    keep_spread(step - 2)
                 if step == 1:
                     quantize(g_q[0], g_s[0], g_in[0])
                 if 0 <= k < K:

@@ -28,6 +28,9 @@ ADJ_ROUND = (0, 2)
 QUANTISE_LAG, RESIDUAL_LAG, STATS_LAG, CENTRE_LAG, FINISH_LAG = 1, 2, 3, 3, 4
 ROUND_BUFS = 4
 LAST_PIECES = 2
+ON_GPSIMD = (4,)
+NORM_ROUND = 8
+STORE_LAG = 1
 
 
 def tile_block_attention_guide_pb_kernel(tc, g1, res1, adj, spatial_adj, conv2_w, conv2_b, s2, norm2_g, norm2_b, out_0, out_1):
@@ -267,17 +270,40 @@ def tile_block_attention_guide_pb_kernel(tc, g1, res1, adj, spatial_adj, conv2_w
             x2, total, negm = live[("x2", b)]
             cen = work.tile([P, C], F32, name="cen", tag="cen")
             nc.vector.scalar_tensor_tensor(
-                out=cen[:], in0=x2[:], scalar=negm[:, 0:1], in1=gam[:], op0=ALU.add, op1=ALU.mult
+                out=cen[:], in0=x2[:], scalar=negm[:, 0:1], in1=live.get(("norm", 0), gam)[:], op0=ALU.add, op1=ALU.mult
             )
             live[("cen", b)] = cen
 
+        def spread_again(which):
+            wide = bank_tile([P, C], F32)
+            nc.tensor.matmul(out=wide[:], lhsT=ones[:], rhs=gb_rows[:, C * which : C * (which + 1)], start=True, stop=True)
+            live[("norm", which)] = wide
+
+        def normalise(b):
+            x2, total, negm = live[("x2", b)]
+            shift = work.tile([P, 1], F32, name="shift", tag="shift")
+            nc.scalar.activation(out=shift[:], in_=negm[:], func=ACT.Copy, scale=live[("rstd", b)][:, 0:1])
+            unit = work.tile([P, C], F32, name="unit", tag="unit")
+            nc.scalar.activation(out=unit[:], in_=x2[:], func=ACT.Identity, bias=shift[:, 0:1], scale=live[("rstd", b)][:, 0:1])
+            live[("unit", b)] = unit
+
+        def finish_on_gpsimd(b):
+            scaled = work.tile([P, C], F32, name="scaled", tag="scaled")
+            xn = work.tile([P, C], F32, name="gxn", tag="gxn")
+            nc.gpsimd.tensor_tensor(out=scaled[:], in0=live[("unit", b)][:], in1=gam[:], op=ALU.mult)
+            nc.gpsimd.tensor_tensor(out=xn[:], in0=scaled[:], in1=bet[:], op=ALU.add)
+            live[("gxn", b)] = xn
+
         def finish(b):
+            for o in ON_GPSIMD:
+                if b == o + STORE_LAG:
+                    nc.sync.dma_start(out=out_1[o], in_=live[("gxn", o)][:])
             xn = work.tile([P, C], F32, name="xn", tag="xn")
             pieces = LAST_PIECES if b == B - 1 else 1
             for piece in range(pieces):
                 cols = slice(C * piece // pieces, C * (piece + 1) // pieces)
                 nc.vector.scalar_tensor_tensor(
-                    out=xn[:, cols], in0=live[("cen", b)][:, cols], scalar=live[("rstd", b)][:, 0:1], in1=bet[:, cols],
+                    out=xn[:, cols], in0=live[("cen", b)][:, cols], scalar=live[("rstd", b)][:, 0:1], in1=live.get(("norm", 1), bet)[:, cols],
                     op0=ALU.mult, op1=ALU.add,
                 )
                 nc.sync.dma_start(out=out_1[b][:, cols], in_=xn[:, cols])
@@ -325,6 +351,9 @@ def tile_block_attention_guide_pb_kernel(tc, g1, res1, adj, spatial_adj, conv2_w
                     weave_adjacency(HALF * (step - len(sources)) + bl)
 
         for rnd in range(B + FINISH_LAG):
+            if rnd == NORM_ROUND:
+                spread_again(0)
+                spread_again(1)
             late = LATE_SLICES[rnd] if rnd < len(LATE_SLICES) else ()
             if rnd < B:
                 for pair in range(2):
@@ -342,14 +371,19 @@ def tile_block_attention_guide_pb_kernel(tc, g1, res1, adj, spatial_adj, conv2_w
                 stage2(rnd - QUANTISE_LAG)
             if 0 <= rnd - STATS_LAG < B:
                 squares(rnd - STATS_LAG)
+                if rnd - STATS_LAG in ON_GPSIMD:
+                    inverse_deviation(rnd - STATS_LAG)
+                    normalise(rnd - STATS_LAG)
+                    finish_on_gpsimd(rnd - STATS_LAG)
             for k in late:
                 for j in range(CHUNKS):
                     empty_bank(k, j, 1)
             if 0 <= rnd - RESIDUAL_LAG < B:
                 residual(rnd - RESIDUAL_LAG)
             if 0 <= rnd - STATS_LAG < B:
-                inverse_deviation(rnd - STATS_LAG)
-            if 0 <= rnd - CENTRE_LAG < B:
+                if rnd - STATS_LAG not in ON_GPSIMD:
+                    inverse_deviation(rnd - STATS_LAG)
+            if 0 <= rnd - CENTRE_LAG < B and rnd - CENTRE_LAG not in ON_GPSIMD:
                 centre(rnd - CENTRE_LAG)
-            if 0 <= rnd - FINISH_LAG < B:
+            if 0 <= rnd - FINISH_LAG < B and rnd - FINISH_LAG not in ON_GPSIMD:
                 finish(rnd - FINISH_LAG)

@@ -47,7 +47,6 @@ def tile_block_attention_guide_pb_kernel(tc, g1, res1, adj, spatial_adj, conv2_w
         res_sb = keep.tile([P, B, C], BF16, name="res_sb")
         b_rows = keep.tile([P, P], F32, name="b_rows")
         bias_w = keep.tile([P, 2 * K], F32, name="bias_w")
-        gb_rows = keep.tile([P, 2 * C], BF16, name="gb_rows")
         gain = keep.tile([P, 1], BF16, name="gain")
         ones = keep.tile([P, P], BF16, name="ones")
         idle = keep.tile([P, C], BF16, name="idle")
@@ -71,12 +70,9 @@ def tile_block_attention_guide_pb_kernel(tc, g1, res1, adj, spatial_adj, conv2_w
 
         nc.vector.memset(idle[:].bitcast(F32), 0.0)
         nc.vector.memset(b_rows[:], 0.0)
-        nc.vector.memset(gb_rows[:].bitcast(F32), 0.0)
         nc.vector.memset(warm[:], 1.0)
         nc.vector.memset(gain[:], 1.0)
         nc.scalar.dma_start(out=b_rows[0 : 2 * K, :].bitcast(BF16), in_=conv2_b.rearrange("(r x) -> r x", x=2 * P))
-        nc.scalar.dma_start(out=gb_rows[0:1, 0:C], in_=norm2_g.rearrange("(o c) -> o c", o=1))
-        nc.scalar.dma_start(out=gb_rows[0:1, C : 2 * C], in_=norm2_b.rearrange("(o c) -> o c", o=1))
         nc.scalar.activation(out=warm2[:], in_=warm[:], func=ACT.Abs_reciprocal_sqrt)
 
         def load_rows(loaded, pair, hbm_rows):
@@ -114,27 +110,22 @@ def tile_block_attention_guide_pb_kernel(tc, g1, res1, adj, spatial_adj, conv2_w
             some = slice(HALF * half, HALF * (half + 1))
             nc.sync.dma_start(out=res_sb[:, some, :], in_=res1[some].rearrange("b w c -> w b c"))
 
+        nc.sync.dma_start(out=gam[:], in_=norm2_g.partition_broadcast(P))
+        nc.sync.dma_start(out=bet[:], in_=norm2_b.partition_broadcast(P))
+
         masks.make_identity(nc, ident_f[:])
         nc.vector.tensor_copy(
             out=perm_f[:].rearrange("p (n u m) -> p n u m", n=2, u=2),
             in_=ident_f[:].rearrange("p (n m u) -> p n u m", n=2, u=2),
         )
 
-        nc.vector.memset(ones[:], 1.0)
+        nc.vector.memset(ones[:], 1.0 / P)
 
         def bank_tile(shape, dtype):
             return psum.tile(shape, dtype, name="ps", tag="ps")
 
         def spin():
             nc.tensor.matmul(out=bank_tile([P, C], F32)[:], lhsT=idle[:, 0:P], rhs=idle[:], start=True, stop=True)
-
-        def spread(which):
-            wide = bank_tile([P, C], F32)
-            nc.tensor.matmul(out=wide[:], lhsT=ones[:], rhs=gb_rows[:, C * which : C * (which + 1)], start=True, stop=True)
-            live[("wide", which)] = wide
-
-        def keep_spread(which):
-            nc.scalar.copy(out=(gam, bet)[which][:], in_=live[("wide", which)][:])
 
         def turn_bias():
             b_t = bank_tile([P, P], F32)
@@ -276,7 +267,7 @@ def tile_block_attention_guide_pb_kernel(tc, g1, res1, adj, spatial_adj, conv2_w
 
         def spread_again(which):
             wide = bank_tile([P, C], F32)
-            nc.tensor.matmul(out=wide[:], lhsT=ones[:], rhs=gb_rows[:, C * which : C * (which + 1)], start=True, stop=True)
+            nc.tensor.matmul(out=wide[:], lhsT=ones[:], rhs=(gam, bet)[which][:], start=True, stop=True)
             live[("norm", which)] = wide
 
         def normalise(b):
@@ -322,9 +313,6 @@ def tile_block_attention_guide_pb_kernel(tc, g1, res1, adj, spatial_adj, conv2_w
                     turn_rows(("turned", step, pair), loaded, matrix, pair)
                 if step == 1:
                     turn_bias()
-                if step == 2:
-                    spread(0)
-                    spread(1)
             if 0 <= k < K:
                 for j in range(CHUNKS):
                     stage1(k, j, 0)
@@ -334,8 +322,6 @@ def tile_block_attention_guide_pb_kernel(tc, g1, res1, adj, spatial_adj, conv2_w
                 if step == 1:
                     keep_bias()
                 empty(("turned", step, 1), grouped, 1, "S")
-                if step in (2, 3):
-                    keep_spread(step - 2)
                 if step == 1:
                     quantize(g_q[0], g_s[0], g_in[0])
                 if 0 <= k < K:

@@ -20,11 +20,17 @@ CHUNKS = 4
 
 FLOPS = 2 * B * J * C * K * C + 2 * B * J * K * J * C
 
-ON_VECTOR = {(0, 0): (0, 3), (0, 1): (0, 3), (1, 0): (1, 2, 3), (1, 1): (0, 1)}
+ON_VECTOR = {(0, 0): (0,), (0, 1): (0, 1), (1, 0): (0, 1), (1, 1): (0, 1, 2)}
 WARM_UP = 4
+ORDER = "TLAQRSCBIF"
+PART_STEPS = {}
+ACC_BANKS = 2
+NORM_BANKS = 0
+BY_GPSIMD = ()
+WEAVE_STEP = {6: (0, 1, 2, 3), 7: (4, 5, 6, 7)}
 LEAD = 2
-LATE_SLICES = ((0, 1), (2,), (3,))
-ADJ_ROUND = (0, 2)
+LATE_SLICES = ((0,), (1,), (2,), (3,))
+ADJ_ROUND = (0, 1)
 QUANTISE_LAG, RESIDUAL_LAG, STATS_LAG, CENTRE_LAG, FINISH_LAG = 1, 2, 3, 3, 4
 ROUND_BUFS = 4
 LAST_PIECES = 2
@@ -38,7 +44,11 @@ def tile_block_attention_guide_pb_kernel(tc, g1, res1, adj, spatial_adj, conv2_w
     with ExitStack() as ctx:
         keep = ctx.enter_context(tc.tile_pool(name="keep", bufs=1))
         work = ctx.enter_context(tc.tile_pool(name="work", bufs=ROUND_BUFS))
-        psum = ctx.enter_context(tc.psum_pool(name="psum", bufs=8))
+        psum = ctx.enter_context(tc.psum_pool(name="psum", bufs=8 - ACC_BANKS - NORM_BANKS))
+        if ACC_BANKS:
+            psum_acc = ctx.enter_context(tc.psum_pool(name="psum_acc", bufs=ACC_BANKS))
+        if NORM_BANKS:
+            psum_norm = ctx.enter_context(tc.psum_pool(name="psum_norm", bufs=NORM_BANKS))
         ctx.enter_context(tc.manual_schedule())
 
         g_sb = [keep.tile([P, HALF, C], BF16, name="g_sb%d" % half) for half in range(2)]
@@ -66,6 +76,9 @@ def tile_block_attention_guide_pb_kernel(tc, g1, res1, adj, spatial_adj, conv2_w
         a_q = [keep.tile([P, HALF * J], U32, name="a_q%d" % half, align_bytes=64) for half in range(2)]
         a_s = [keep.tile([P, HALF * J], U8, name="a_s%d" % half, align_bytes=64) for half in range(2)]
         h_t = [[keep.tile([P, HALF * C], BF16, name="h_t%d_%d" % (half, j)) for j in range(CHUNKS)] for half in range(2)]
+        parted = {}
+        for index in PART_STEPS:
+            parted[index] = keep.tile([P, CHUNKS, C], BF16, name="parted%d" % index)
         live = {}
 
         nc.vector.memset(idle[:].bitcast(F32), 0.0)
@@ -122,6 +135,12 @@ def tile_block_attention_guide_pb_kernel(tc, g1, res1, adj, spatial_adj, conv2_w
         nc.vector.memset(ones[:], 1.0 / P)
 
         def bank_tile(shape, dtype):
+            live["n"] = live.get("n", -1) + 1
+            turn = live["n"] % (8 - ACC_BANKS if live.get("rounds") else 8)
+            if turn >= 8 - ACC_BANKS:
+                return psum_acc.tile(shape, dtype, name="pa", tag="pa")
+            if turn >= 8 - ACC_BANKS - NORM_BANKS and ("norm", 0) not in live:
+                return psum_norm.tile(shape, dtype, name="pn", tag="pn")
             return psum.tile(shape, dtype, name="ps", tag="ps")
 
         def spin():
@@ -141,12 +160,21 @@ def tile_block_attention_guide_pb_kernel(tc, g1, res1, adj, spatial_adj, conv2_w
             else:
                 nc.scalar.copy(out=dst, in_=src)
 
+        def part_words(index, eng):
+            loaded = raw[index]
+            for pair in range(2):
+                some = slice(2 * pair, 2 * pair + 2)
+                (nc.vector.tensor_copy if eng == "V" else nc.scalar.copy)(
+                    out=parted[index][:, some, :].bitcast(F32).rearrange("p a (u w) -> p a u w", u=2),
+                    in_=loaded[:, some, :].bitcast(F32).rearrange("p a (w u) -> p a u w", u=2),
+                )
+
         def turn_rows(key, loaded, matrix, pair):
             tr = bank_tile([P, 2, 2, P], F32)
             for a in range(2):
                 words = loaded[:, 2 * pair + a, :].bitcast(F32)
                 for u in range(2):
-                    nc.tensor.transpose(tr[:, a, u, :], words[:, u::2], matrix[:])
+                    nc.tensor.transpose(tr[:, a, u, :], words[:, P * u : P * (u + 1)] if loaded in list(parted.values()) else words[:, u::2], matrix[:])
             live[key] = tr
 
         def empty_slots(key, grouped, pair, eng):
@@ -216,7 +244,7 @@ def tile_block_attention_guide_pb_kernel(tc, g1, res1, adj, spatial_adj, conv2_w
         def stage2(b):
             half, bl = divmod(b, HALF)
             h_q, h_s = live[("h_q", b)]
-            acc = bank_tile([P, C], F32)
+            acc = psum_acc.tile([P, C], F32, name="pa", tag="pa") if ACC_BANKS else bank_tile([P, C], F32)
             cols = slice(J * bl, J * (bl + 1))
             nc.tensor.matmul_mx(
                 out=acc[:],
@@ -266,16 +294,19 @@ def tile_block_attention_guide_pb_kernel(tc, g1, res1, adj, spatial_adj, conv2_w
             live[("cen", b)] = cen
 
         def spread_again(which):
-            wide = bank_tile([P, C], F32)
+            wide = psum_norm.tile([P, C], F32, name="pn", tag="pn") if NORM_BANKS else bank_tile([P, C], F32)
             nc.tensor.matmul(out=wide[:], lhsT=ones[:], rhs=(gam, bet)[which][:], start=True, stop=True)
             live[("norm", which)] = wide
 
         def normalise(b):
             x2, total, negm = live[("x2", b)]
-            shift = work.tile([P, 1], F32, name="shift", tag="shift")
-            nc.scalar.activation(out=shift[:], in_=negm[:], func=ACT.Copy, scale=live[("rstd", b)][:, 0:1])
             unit = work.tile([P, C], F32, name="unit", tag="unit")
-            nc.scalar.activation(out=unit[:], in_=x2[:], func=ACT.Identity, bias=shift[:, 0:1], scale=live[("rstd", b)][:, 0:1])
+            if b in BY_GPSIMD:
+                nc.gpsimd.tensor_scalar(out=unit[:], in0=x2[:], scalar1=negm[:, 0:1], scalar2=live[("rstd", b)][:, 0:1], op0=ALU.add, op1=ALU.mult)
+            else:
+                shift = work.tile([P, 1], F32, name="shift", tag="shift")
+                nc.scalar.activation(out=shift[:], in_=negm[:], func=ACT.Copy, scale=live[("rstd", b)][:, 0:1])
+                nc.scalar.activation(out=unit[:], in_=x2[:], func=ACT.Identity, bias=shift[:, 0:1], scale=live[("rstd", b)][:, 0:1])
             live[("unit", b)] = unit
 
         def finish_on_gpsimd(b):
@@ -286,9 +317,6 @@ def tile_block_attention_guide_pb_kernel(tc, g1, res1, adj, spatial_adj, conv2_w
             live[("gxn", b)] = xn
 
         def finish(b):
-            for o in ON_GPSIMD:
-                if b == o + STORE_LAG:
-                    nc.sync.dma_start(out=out_1[o], in_=live[("gxn", o)][:])
             xn = work.tile([P, C], F32, name="xn", tag="xn")
             pieces = LAST_PIECES if b == B - 1 else 1
             for piece in range(pieces):
@@ -298,6 +326,9 @@ def tile_block_attention_guide_pb_kernel(tc, g1, res1, adj, spatial_adj, conv2_w
                     op0=ALU.mult, op1=ALU.add,
                 )
                 nc.sync.dma_start(out=out_1[b][:, cols], in_=xn[:, cols])
+            if b == B - 1:
+                for o in ON_GPSIMD:
+                    nc.scalar.dma_start(out=out_1[o], in_=live[("gxn", o)][:])
 
         for step in range(WARM_UP):
             spin()
@@ -305,13 +336,19 @@ def tile_block_attention_guide_pb_kernel(tc, g1, res1, adj, spatial_adj, conv2_w
         sources = [(g_sb[0], perm_f, empty_woven, g_in[0], g_q[0], g_s[0])]
         sources += [(w_sb[k], ident_f, empty_slots, w_in[k], w_q[k], w_s[k]) for k in range(K)]
         sources += [(g_sb[1], perm_f, empty_woven, g_in[1], g_q[1], g_s[1])]
+        raw = [source[0] for source in sources]
+        for index in PART_STEPS:
+            sources[index] = (parted[index],) + sources[index][1:]
         for step in range(len(sources) + LEAD):
+            for index in PART_STEPS:
+                if PART_STEPS[index] == (PART_STEPS[index][0], step, "pre"):
+                    part_words(index, PART_STEPS[index][0])
             k = step - 1 - LEAD
             if step < len(sources):
                 loaded, matrix, empty, grouped, codes, scales = sources[step]
                 for pair in range(2):
                     turn_rows(("turned", step, pair), loaded, matrix, pair)
-                if step == 1:
+                if step == 2:
                     turn_bias()
             if 0 <= k < K:
                 for j in range(CHUNKS):
@@ -319,9 +356,12 @@ def tile_block_attention_guide_pb_kernel(tc, g1, res1, adj, spatial_adj, conv2_w
             emptied = 0
             if step < len(sources):
                 empty(("turned", step, 0), grouped, 0, "V")
-                if step == 1:
+                if step == 2:
                     keep_bias()
                 empty(("turned", step, 1), grouped, 1, "S")
+                for index in PART_STEPS:
+                    if PART_STEPS[index] == (PART_STEPS[index][0], step, "mid"):
+                        part_words(index, PART_STEPS[index][0])
                 if step == 1:
                     quantize(g_q[0], g_s[0], g_in[0])
                 if 0 <= k < K:
@@ -332,44 +372,47 @@ def tile_block_attention_guide_pb_kernel(tc, g1, res1, adj, spatial_adj, conv2_w
             if 0 <= k < K:
                 for j in range(emptied, CHUNKS):
                     empty_bank(k, j, 0)
-            if step >= len(sources):
-                for bl in range(HALF):
-                    weave_adjacency(HALF * (step - len(sources)) + bl)
+            for b in WEAVE_STEP.get(step, ()):
+                weave_adjacency(b)
 
+        live["rounds"] = True
         for rnd in range(B + FINISH_LAG):
             if rnd == NORM_ROUND:
                 spread_again(0)
                 spread_again(1)
             late = LATE_SLICES[rnd] if rnd < len(LATE_SLICES) else ()
-            if rnd < B:
-                for pair in range(2):
-                    turn_h(rnd, pair)
-                for pair in range(2):
-                    empty_h(rnd, pair)
-            for k in late:
-                for j in range(CHUNKS):
-                    stage1(k, j, 1)
-            for half in range(2):
-                if ADJ_ROUND[half] == rnd:
-                    quantize(a_q[half], a_s[half], a_in[half])
-            if 0 <= rnd - QUANTISE_LAG < B:
-                quantize_h(rnd - QUANTISE_LAG)
-                stage2(rnd - QUANTISE_LAG)
-            if 0 <= rnd - STATS_LAG < B:
-                squares(rnd - STATS_LAG)
-                if rnd - STATS_LAG in ON_GPSIMD:
+            for token in ORDER:
+                if token == "T" and rnd < B:
+                    for pair in range(2):
+                        turn_h(rnd, pair)
+                    for pair in range(2):
+                        empty_h(rnd, pair)
+                if token == "L":
+                    for k in late:
+                        for j in range(CHUNKS):
+                            stage1(k, j, 1)
+                if token == "A":
+                    for half in range(2):
+                        if ADJ_ROUND[half] == rnd:
+                            quantize(a_q[half], a_s[half], a_in[half])
+                if token == "Q" and 0 <= rnd - QUANTISE_LAG < B:
+                    quantize_h(rnd - QUANTISE_LAG)
+                    stage2(rnd - QUANTISE_LAG)
+                if token == "S" and 0 <= rnd - STATS_LAG < B:
+                    squares(rnd - STATS_LAG)
+                    if rnd - STATS_LAG in ON_GPSIMD:
+                        inverse_deviation(rnd - STATS_LAG)
+                        normalise(rnd - STATS_LAG)
+                        finish_on_gpsimd(rnd - STATS_LAG)
+                if token == "B":
+                    for k in late:
+                        for j in range(CHUNKS):
+                            empty_bank(k, j, 1)
+                if token == "R" and 0 <= rnd - RESIDUAL_LAG < B:
+                    residual(rnd - RESIDUAL_LAG)
+                if token == "I" and 0 <= rnd - STATS_LAG < B and rnd - STATS_LAG not in ON_GPSIMD:
                     inverse_deviation(rnd - STATS_LAG)
-                    normalise(rnd - STATS_LAG)
-                    finish_on_gpsimd(rnd - STATS_LAG)
-            for k in late:
-                for j in range(CHUNKS):
-                    empty_bank(k, j, 1)
-            if 0 <= rnd - RESIDUAL_LAG < B:
-                residual(rnd - RESIDUAL_LAG)
-            if 0 <= rnd - STATS_LAG < B:
-                if rnd - STATS_LAG not in ON_GPSIMD:
-                    inverse_deviation(rnd - STATS_LAG)
-            if 0 <= rnd - CENTRE_LAG < B and rnd - CENTRE_LAG not in ON_GPSIMD:
-                centre(rnd - CENTRE_LAG)
-            if 0 <= rnd - FINISH_LAG < B and rnd - FINISH_LAG not in ON_GPSIMD:
-                finish(rnd - FINISH_LAG)
+                if token == "C" and 0 <= rnd - CENTRE_LAG < B and rnd - CENTRE_LAG not in ON_GPSIMD:
+                    centre(rnd - CENTRE_LAG)
+                if token == "F" and 0 <= rnd - FINISH_LAG < B and rnd - FINISH_LAG not in ON_GPSIMD:
+                    finish(rnd - FINISH_LAG)

from contextlib import ExitStack

import concourse.masks as masks
import concourse.mybir as mybir

F32 = mybir.dt.float32
BF16 = mybir.dt.bfloat16
U32 = mybir.dt.uint32
U8 = mybir.dt.uint8
FP8X4 = mybir.dt.float8_e4m3fn_x4
ALU = mybir.AluOpType
ACT = mybir.ActivationFunctionType

B, J, C, K = 8, 128, 512, 4
EPS = 1e-5
P = 128
HALF = 4
QUAD = J // 4
CHUNKS = 4

FLOPS = 2 * B * J * C * K * C + 2 * B * J * K * J * C

ON_VECTOR = {(0, 0): (0,), (0, 1): (0, 1), (1, 0): (0, 1), (1, 1): (0, 1, 2)}
WARM_UP = 4
ORDER = "TLAQRSCBIF"
PART_STEPS = {}
ACC_BANKS = 2
NORM_BANKS = 0
BY_GPSIMD = ()
WEAVE_STEP = {6: (0, 1, 2, 3), 7: (4, 5, 6, 7)}
LEAD = 2
LATE_SLICES = ((0,), (1,), (2,), (3,))
ADJ_ROUND = (0, 1)
QUANTISE_LAG, RESIDUAL_LAG, STATS_LAG, CENTRE_LAG, FINISH_LAG = 1, 2, 3, 3, 4
ROUND_BUFS = 4
LAST_PIECES = 2
ON_GPSIMD = (4,)
NORM_ROUND = 8
STORE_LAG = 1


def tile_block_attention_guide_pb_kernel(tc, g1, res1, adj, spatial_adj, conv2_w, conv2_b, s2, norm2_g, norm2_b, out_0, out_1):
    nc = tc.nc
    with ExitStack() as ctx:
        keep = ctx.enter_context(tc.tile_pool(name="keep", bufs=1))
        work = ctx.enter_context(tc.tile_pool(name="work", bufs=ROUND_BUFS))
        psum = ctx.enter_context(tc.psum_pool(name="psum", bufs=8 - ACC_BANKS - NORM_BANKS))
        if ACC_BANKS:
            psum_acc = ctx.enter_context(tc.psum_pool(name="psum_acc", bufs=ACC_BANKS))
        if NORM_BANKS:
            psum_norm = ctx.enter_context(tc.psum_pool(name="psum_norm", bufs=NORM_BANKS))
        ctx.enter_context(tc.manual_schedule())

        g_sb = [keep.tile([P, HALF, C], BF16, name="g_sb%d" % half) for half in range(2)]
        w_sb = [keep.tile([P, CHUNKS, C], BF16, name="w_sb%d" % k) for k in range(K)]
        a_raw = keep.tile([P, B, 4, J], BF16, name="a_raw")
        res_sb = keep.tile([P, B, C], BF16, name="res_sb")
        b_rows = keep.tile([P, P], F32, name="b_rows")
        bias_w = keep.tile([P, 2 * K], F32, name="bias_w")
        gain = keep.tile([P, 1], BF16, name="gain")
        ones = keep.tile([P, P], BF16, name="ones")
        idle = keep.tile([P, C], BF16, name="idle")
        warm = keep.tile([P, 1], F32, name="warm")
        warm2 = keep.tile([P, 1], F32, name="warm2")
        gam = keep.tile([P, C], BF16, name="gam")
        bet = keep.tile([P, C], BF16, name="bet")
        ident_f = keep.tile([P, P], F32, name="ident_f")
        perm_f = keep.tile([P, P], F32, name="perm_f")
        g_in = [keep.tile([P, 4 * C], BF16, name="g_in%d" % half, align_bytes=64) for half in range(2)]
        g_q = [keep.tile([P, C], U32, name="g_q%d" % half, align_bytes=64) for half in range(2)]
        g_s = [keep.tile([P, C], U8, name="g_s%d" % half, align_bytes=64) for half in range(2)]
        w_in = [keep.tile([P, 4 * C], BF16, name="w_in%d" % k, align_bytes=64) for k in range(K)]
        w_q = [keep.tile([P, C], U32, name="w_q%d" % k, align_bytes=64) for k in range(K)]
        w_s = [keep.tile([P, C], U8, name="w_s%d" % k, align_bytes=64) for k in range(K)]
        a_in = [keep.tile([P, HALF * J * 4], BF16, name="a_in%d" % half, align_bytes=64) for half in range(2)]
        a_q = [keep.tile([P, HALF * J], U32, name="a_q%d" % half, align_bytes=64) for half in range(2)]
        a_s = [keep.tile([P, HALF * J], U8, name="a_s%d" % half, align_bytes=64) for half in range(2)]
        h_t = [[keep.tile([P, HALF * C], BF16, name="h_t%d_%d" % (half, j)) for j in range(CHUNKS)] for half in range(2)]
        parted = {}
        for index in PART_STEPS:
            parted[index] = keep.tile([P, CHUNKS, C], BF16, name="parted%d" % index)
        live = {}

        nc.vector.memset(idle[:].bitcast(F32), 0.0)
        nc.vector.memset(b_rows[:], 0.0)
        nc.vector.memset(warm[:], 1.0)
        nc.vector.memset(gain[:], 1.0)
        nc.scalar.dma_start(out=b_rows[0 : 2 * K, :].bitcast(BF16), in_=conv2_b.rearrange("(r x) -> r x", x=2 * P))
        nc.scalar.activation(out=warm2[:], in_=warm[:], func=ACT.Abs_reciprocal_sqrt)

        def load_rows(loaded, pair, hbm_rows):
            nc.sync.dma_start(
                out=loaded[:, 2 * pair : 2 * pair + 2, :].rearrange("p (o a) c -> p o (a c)", a=2),
                in_=hbm_rows.rearrange("(o p a) c -> p o (a c)", p=P, a=2),
            )

        def load_g(half):
            for pair in range(2):
                sample = HALF * half + 2 * pair
                load_rows(g_sb[half], pair, g1[sample : sample + 2].rearrange("b v c -> (b v) c"))

        def load_w(k):
            for pair in range(2):
                row = C * k + 2 * P * pair
                load_rows(w_sb[k], pair, conv2_w[row : row + 2 * P, :])

        def load_adjacency(half):
            some = slice(HALF * half, HALF * (half + 1))
            nc.sync.dma_start(
                out=a_raw[QUAD:P, some].rearrange("p b t w -> p b (t w)"),
                in_=spatial_adj.rearrange("k (m t) w -> (k m) (t w)", t=4).unsqueeze(1).to_broadcast([P - QUAD, HALF, 4 * J]),
            )
            nc.sync.dma_start(out=a_raw[0:QUAD, some], in_=adj[some].rearrange("b o (m t) w -> m (b o) t w", t=4))

        load_g(0)
        for k in range(K):
            load_w(k)
        load_g(1)
        nc.sync.dma_start(out=gain[0:QUAD, :], in_=s2.partition_broadcast(QUAD))
        for half in range(2):
            load_adjacency(half)
        for half in range(2):
            some = slice(HALF * half, HALF * (half + 1))
            nc.sync.dma_start(out=res_sb[:, some, :], in_=res1[some].rearrange("b w c -> w b c"))

        nc.sync.dma_start(out=gam[:], in_=norm2_g.partition_broadcast(P))
        nc.sync.dma_start(out=bet[:], in_=norm2_b.partition_broadcast(P))

        masks.make_identity(nc, ident_f[:])
        nc.vector.tensor_copy(
            out=perm_f[:].rearrange("p (n u m) -> p n u m", n=2, u=2),
            in_=ident_f[:].rearrange("p (n m u) -> p n u m", n=2, u=2),
        )

        nc.vector.memset(ones[:], 1.0 / P)

        def bank_tile(shape, dtype):
            live["n"] = live.get("n", -1) + 1
            turn = live["n"] % (8 - ACC_BANKS if live.get("rounds") else 8)
            if turn >= 8 - ACC_BANKS:
                return psum_acc.tile(shape, dtype, name="pa", tag="pa")
            if turn >= 8 - ACC_BANKS - NORM_BANKS and ("norm", 0) not in live:
                return psum_norm.tile(shape, dtype, name="pn", tag="pn")
            return psum.tile(shape, dtype, name="ps", tag="ps")

        def spin():
            nc.tensor.matmul(out=bank_tile([P, C], F32)[:], lhsT=idle[:, 0:P], rhs=idle[:], start=True, stop=True)

        def turn_bias():
            b_t = bank_tile([P, P], F32)
            nc.tensor.transpose(b_t[:], b_rows[:], ident_f[:])
            live["b_t"] = b_t

        def keep_bias():
            nc.vector.tensor_copy(out=bias_w[:], in_=live["b_t"][:, 0 : 2 * K])

        def copy_words(eng, dst, src):
            if eng == "V":
                nc.vector.tensor_copy(out=dst, in_=src)
            else:
                nc.scalar.copy(out=dst, in_=src)

        def part_words(index, eng):
            loaded = raw[index]
            for pair in range(2):
                some = slice(2 * pair, 2 * pair + 2)
                (nc.vector.tensor_copy if eng == "V" else nc.scalar.copy)(
                    out=parted[index][:, some, :].bitcast(F32).rearrange("p a (u w) -> p a u w", u=2),
                    in_=loaded[:, some, :].bitcast(F32).rearrange("p a (w u) -> p a u w", u=2),
                )

        def turn_rows(key, loaded, matrix, pair):
            tr = bank_tile([P, 2, 2, P], F32)
            for a in range(2):
                words = loaded[:, 2 * pair + a, :].bitcast(F32)
                for u in range(2):
                    nc.tensor.transpose(tr[:, a, u, :], words[:, P * u : P * (u + 1)] if loaded in list(parted.values()) else words[:, u::2], matrix[:])
            live[key] = tr

        def empty_slots(key, grouped, pair, eng):
            dst = grouped[:].bitcast(F32).rearrange("p (a r u) -> p a r u", a=4, u=2)
            copy_words(eng, dst[:, 2 * pair : 2 * pair + 2], live[key][:].rearrange("p a u r -> p a r u"))

        def empty_woven(key, grouped, pair, eng):
            dst = grouped[:].bitcast(F32).rearrange("p (o r a u) -> p o r a u", o=2, a=2, u=2)
            copy_words(eng, dst[:, pair], live[key][:].rearrange("p a u r -> p r a u"))

        def quantize(codes, scales, grouped):
            nc.vector.quantize_mx(out=codes[:].bitcast(FP8X4), scales=scales[:], in_=grouped[:])

        def stage1(k, j, half):
            bank = bank_tile([P, HALF * J], BF16)
            cols = slice(P * j, P * (j + 1))
            nc.tensor.matmul_mx(
                out=bank[:],
                lhsT=w_q[k][:, cols].bitcast(FP8X4),
                lhsT_scale=w_s[k][:, cols],
                rhs=g_q[half][:].bitcast(FP8X4),
                rhs_scale=g_s[half][:],
                start=True,
                stop=True,
            )
            live[("bank", k, j, half)] = bank

        def empty_bank(k, j, half):
            dst = h_t[half][j][:].rearrange("p (b u k x) -> p b u k x", b=HALF, u=2, k=K)[:, :, :, k, :]
            src = live[("bank", k, j, half)][:].rearrange("p (b u x) -> p b u x", b=HALF, u=2)
            col = bias_w[:].bitcast(BF16)[:, CHUNKS * k + j : CHUNKS * k + j + 1]
            if j in ON_VECTOR[(half, k % 2)]:
                nc.vector.tensor_scalar(out=dst, in0=src, scalar1=col, scalar2=None, op0=ALU.add)
            else:
                nc.scalar.activation(out=dst, in_=src, func=ACT.Identity, bias=col, scale=1.0)

        def turn_h(b, pair):
            half, bl = divmod(b, HALF)
            tr = bank_tile([P, 2, 2, P], F32)
            for a in range(2):
                chunk = h_t[half][2 * pair + a][:].rearrange("p (b u x) -> p b u x", b=HALF, u=2)
                for u in range(2):
                    nc.tensor.transpose(tr[:, a, u, :], chunk[:, bl, u, :].bitcast(F32), ident_f[:])
            live[("h", b, pair)] = tr

        def empty_h(b, pair):
            if pair == 0:
                live[("h_in", b)] = work.tile([P, 4 * C], BF16, name="h_in", tag="h_in", align_bytes=64)
            empty_woven(("h", b, pair), live[("h_in", b)], pair, "S")

        def quantize_h(b):
            h_q = work.tile([P, C], U32, name="h_q", tag="h_q", align_bytes=64)
            h_s = work.tile([P, C], U8, name="h_s", tag="h_s", align_bytes=64)
            quantize(h_q, h_s, live[("h_in", b)])
            live[("h_q", b)] = (h_q, h_s)

        def weave_adjacency(b):
            half, bl = divmod(b, HALF)
            nc.vector.tensor_scalar(
                out=a_in[half][:].rearrange("p (b c i t) -> p b c t i", b=HALF, i=4, t=4)[:, bl],
                in0=a_raw[:, b].rearrange("p t (c i) -> p c t i", i=4),
                scalar1=gain[:, 0:1],
                scalar2=None,
                op0=ALU.mult,
            )

        def stage2(b):
            half, bl = divmod(b, HALF)
            h_q, h_s = live[("h_q", b)]
            acc = psum_acc.tile([P, C], F32, name="pa", tag="pa") if ACC_BANKS else bank_tile([P, C], F32)
            cols = slice(J * bl, J * (bl + 1))
            nc.tensor.matmul_mx(
                out=acc[:],
                lhsT=a_q[half][:, cols].bitcast(FP8X4),
                lhsT_scale=a_s[half][:, cols],
                rhs=h_q[:].bitcast(FP8X4),
                rhs_scale=h_s[:],
                start=True,
                stop=True,
            )
            live[("acc", b)] = acc

        def residual(b):
            x2 = work.tile([P, C], F32, name="x2", tag="x2")
            total = work.tile([P, 1], F32, name="total", tag="total")
            nc.vector.scalar_tensor_tensor(
                out=x2[:], in0=live[("acc", b)][:], scalar=1.0, in1=res_sb[:, b, :],
                op0=ALU.mult, op1=ALU.add, accum_out=total[:],
            )
            nc.sync.dma_start(out=out_0[b], in_=x2[:])
            negm = work.tile([P, 1], F32, name="negm", tag="negm")
            nc.scalar.activation(out=negm[:], in_=total[:], func=ACT.Copy, scale=-1.0 / C)
            live[("x2", b)] = (x2, total, negm)

        def squares(b):
            x2, total, negm = live[("x2", b)]
            junk = work.tile([P, C], BF16, name="junk", tag="junk")
            ssq = work.tile([P, 1], F32, name="ssq", tag="ssq")
            nc.scalar.activation(
                out=junk[:], in_=x2[:], func=ACT.Square, bias=total[:, 0:1], scale=-1.0 * C, accum_out=ssq[:]
            )
            live[("ssq", b)] = ssq

        def inverse_deviation(b):
            rstd = work.tile([P, 1], F32, name="rstd", tag="rstd")
            nc.scalar.activation(
                out=rstd[:], in_=live[("ssq", b)][:], func=ACT.Abs_reciprocal_sqrt, bias=EPS, scale=1.0 / (C * C * C)
            )
            live[("rstd", b)] = rstd

        def centre(b):
            x2, total, negm = live[("x2", b)]
            cen = work.tile([P, C], F32, name="cen", tag="cen")
            nc.vector.scalar_tensor_tensor(
                out=cen[:], in0=x2[:], scalar=negm[:, 0:1], in1=live.get(("norm", 0), gam)[:], op0=ALU.add, op1=ALU.mult
            )
            live[("cen", b)] = cen

        def spread_again(which):
            wide = psum_norm.tile([P, C], F32, name="pn", tag="pn") if NORM_BANKS else bank_tile([P, C], F32)
            nc.tensor.matmul(out=wide[:], lhsT=ones[:], rhs=(gam, bet)[which][:], start=True, stop=True)
            live[("norm", which)] = wide

        def normalise(b):
            x2, total, negm = live[("x2", b)]
            unit = work.tile([P, C], F32, name="unit", tag="unit")
            if b in BY_GPSIMD:
                nc.gpsimd.tensor_scalar(out=unit[:], in0=x2[:], scalar1=negm[:, 0:1], scalar2=live[("rstd", b)][:, 0:1], op0=ALU.add, op1=ALU.mult)
            else:
                shift = work.tile([P, 1], F32, name="shift", tag="shift")
                nc.scalar.activation(out=shift[:], in_=negm[:], func=ACT.Copy, scale=live[("rstd", b)][:, 0:1])
                nc.scalar.activation(out=unit[:], in_=x2[:], func=ACT.Identity, bias=shift[:, 0:1], scale=live[("rstd", b)][:, 0:1])
            live[("unit", b)] = unit

        def finish_on_gpsimd(b):
            scaled = work.tile([P, C], F32, name="scaled", tag="scaled")
            xn = work.tile([P, C], F32, name="gxn", tag="gxn")
            nc.gpsimd.tensor_tensor(out=scaled[:], in0=live[("unit", b)][:], in1=gam[:], op=ALU.mult)
            nc.gpsimd.tensor_tensor(out=xn[:], in0=scaled[:], in1=bet[:], op=ALU.add)
            live[("gxn", b)] = xn

        def finish(b):
            xn = work.tile([P, C], F32, name="xn", tag="xn")
            pieces = LAST_PIECES if b == B - 1 else 1
            for piece in range(pieces):
                cols = slice(C * piece // pieces, C * (piece + 1) // pieces)
                nc.vector.scalar_tensor_tensor(
                    out=xn[:, cols], in0=live[("cen", b)][:, cols], scalar=live[("rstd", b)][:, 0:1], in1=live.get(("norm", 1), bet)[:, cols],
                    op0=ALU.mult, op1=ALU.add,
                )
                nc.sync.dma_start(out=out_1[b][:, cols], in_=xn[:, cols])
            if b == B - 1:
                for o in ON_GPSIMD:
                    nc.scalar.dma_start(out=out_1[o], in_=live[("gxn", o)][:])

        for step in range(WARM_UP):
            spin()

        sources = [(g_sb[0], perm_f, empty_woven, g_in[0], g_q[0], g_s[0])]
        sources += [(w_sb[k], ident_f, empty_slots, w_in[k], w_q[k], w_s[k]) for k in range(K)]
        sources += [(g_sb[1], perm_f, empty_woven, g_in[1], g_q[1], g_s[1])]
        raw = [source[0] for source in sources]
        for index in PART_STEPS:
            sources[index] = (parted[index],) + sources[index][1:]
        for step in range(len(sources) + LEAD):
            for index in PART_STEPS:
                if PART_STEPS[index] == (PART_STEPS[index][0], step, "pre"):
                    part_words(index, PART_STEPS[index][0])
            k = step - 1 - LEAD
            if step < len(sources):
                loaded, matrix, empty, grouped, codes, scales = sources[step]
                for pair in range(2):
                    turn_rows(("turned", step, pair), loaded, matrix, pair)
                if step == 2:
                    turn_bias()
            if 0 <= k < K:
                for j in range(CHUNKS):
                    stage1(k, j, 0)
            emptied = 0
            if step < len(sources):
                empty(("turned", step, 0), grouped, 0, "V")
                if step == 2:
                    keep_bias()
                empty(("turned", step, 1), grouped, 1, "S")
                for index in PART_STEPS:
                    if PART_STEPS[index] == (PART_STEPS[index][0], step, "mid"):
                        part_words(index, PART_STEPS[index][0])
                if step == 1:
                    quantize(g_q[0], g_s[0], g_in[0])
                if 0 <= k < K:
                    empty_bank(k, 0, 0)
                    emptied = 1
                if step > 0:
                    quantize(codes, scales, grouped)
            if 0 <= k < K:
                for j in range(emptied, CHUNKS):
                    empty_bank(k, j, 0)
            for b in WEAVE_STEP.get(step, ()):
                weave_adjacency(b)

        live["rounds"] = True
        for rnd in range(B + FINISH_LAG):
            if rnd == NORM_ROUND:
                spread_again(0)
                spread_again(1)
            late = LATE_SLICES[rnd] if rnd < len(LATE_SLICES) else ()
            for token in ORDER:
                if token == "T" and rnd < B:
                    for pair in range(2):
                        turn_h(rnd, pair)
                    for pair in range(2):
                        empty_h(rnd, pair)
                if token == "L":
                    for k in late:
                        for j in range(CHUNKS):
                            stage1(k, j, 1)
                if token == "A":
                    for half in range(2):
                        if ADJ_ROUND[half] == rnd:
                            quantize(a_q[half], a_s[half], a_in[half])
                if token == "Q" and 0 <= rnd - QUANTISE_LAG < B:
                    quantize_h(rnd - QUANTISE_LAG)
                    stage2(rnd - QUANTISE_LAG)
                if token == "S" and 0 <= rnd - STATS_LAG < B:
                    squares(rnd - STATS_LAG)
                    if rnd - STATS_LAG in ON_GPSIMD:
                        inverse_deviation(rnd - STATS_LAG)
                        normalise(rnd - STATS_LAG)
                        finish_on_gpsimd(rnd - STATS_LAG)
                if token == "B":
                    for k in late:
                        for j in range(CHUNKS):
                            empty_bank(k, j, 1)
                if token == "R" and 0 <= rnd - RESIDUAL_LAG < B:
                    residual(rnd - RESIDUAL_LAG)
                if token == "I" and 0 <= rnd - STATS_LAG < B and rnd - STATS_LAG not in ON_GPSIMD:
                    inverse_deviation(rnd - STATS_LAG)
                if token == "C" and 0 <= rnd - CENTRE_LAG < B and rnd - CENTRE_LAG not in ON_GPSIMD:
                    centre(rnd - CENTRE_LAG)
                if token == "F" and 0 <= rnd - FINISH_LAG < B and rnd - FINISH_LAG not in ON_GPSIMD:
                    finish(rnd - FINISH_LAG)
